import numpy as np
import ml_dtypes


def mxq(x, axis, fmt="e4m3"):
    dtype, down = {"e4m3": (ml_dtypes.float8_e4m3fn, 7), "e5m2": (ml_dtypes.float8_e5m2, 14)}[fmt]
    v = np.moveaxis(np.asarray(x, np.float32).astype(ml_dtypes.bfloat16).astype(np.float64), axis, -1)
    blocks = v.reshape(v.shape[:-1] + (-1, 32))
    amax = np.abs(blocks).max(-1, keepdims=True)
    byte = np.maximum(np.where(amax > 0, np.frexp(amax)[1] - 1 + 127, 0) - down, 1)
    scale = np.exp2(byte - 127.0)
    codes = (blocks / scale).astype(np.float32).astype(dtype).astype(np.float64)
    return np.moveaxis((codes * scale).reshape(v.shape), -1, axis)


WIDE = False


def mx_kscale(k):
    if not WIDE:
        return np.ones(k)
    levels = np.array([10, -10, 5, -5, 0])
    a = np.random.permutation(np.resize(levels, k // 512 * 4)).reshape(k // 512, 4)
    idx = np.arange(k)
    return np.exp2(a[idx // 512, idx % 128 // 32])


BF16 = ml_dtypes.bfloat16


def bf(x):
    return np.asarray(x, np.float32).astype(BF16)


def f64(x):
    return np.asarray(x).astype(np.float64)


B, N, ATTR, STATE, REL, G, NF = 4, 64, 4, 16, 9, 32, 512


def setup_inputs():
    rn = np.random.standard_normal
    s, u, t = mx_kscale(NF), mx_kscale(NF), mx_kscale(NF)
    rp_rows = np.concatenate([s, u, u])
    pp_rows = np.concatenate([u, t])
    pp_scale = np.concatenate([np.full(NF, 1.0 / np.sqrt(NF)), np.full(NF, 1.0 / np.sqrt(NF * N))])
    return {
        "rel_enc": bf(np.maximum(rn((B, N, N, NF)) * 1.1, 0.0) * s),
        "obj": bf(np.maximum(rn((B, N, NF)) * 1.1, 0.0) * u),
        "rp_w": bf(rn((3 * NF, NF)) * 2.0 / np.sqrt(3 * NF * N) / rp_rows[:, None] * t),
        "rp_b": bf(rn(NF) * 0.1 * t),
        "pp_w": bf(rn((2 * NF, NF)) * (pp_scale / pp_rows)[:, None]),
        "pp_b": bf(rn(NF) * 0.1),
    }


def reference(rel_enc, obj, rp_w, rp_b, pp_w, pp_b):
    rp, pp = f64(rp_w), f64(pp_w)
    oq = mxq(f64(obj), 2, "e4m3")
    e_rel = mxq(f64(rel_enc), 3, "e4m3") @ mxq(rp[:NF], 0, "e4m3")
    e_recv = oq @ mxq(rp[NF:2 * NF], 0, "e4m3")
    e_send = oq @ mxq(rp[2 * NF:], 0, "e4m3")
    rel_eff = np.maximum(e_rel + e_recv[:, :, None, :] + e_send[:, None, :, :] + f64(rp_b), 0.0)
    agg = rel_eff.sum(axis=2)
    p_obj = oq @ mxq(pp[:NF], 0, "e4m3")
    p_agg = mxq(agg, 2, "e4m3") @ mxq(pp[NF:], 0, "e4m3")
    return np.maximum(p_obj + p_agg + f64(pp_b), 0.0)

@@ -1,0 +1,318 @@
+from contextlib import ExitStack
+
+import concourse.mybir as mybir
+from concourse.masks import make_identity
+
+F32 = mybir.dt.float32
+BF16 = mybir.dt.bfloat16
+U32 = mybir.dt.uint32
+U8 = mybir.dt.uint8
+FP8X4 = mybir.dt.float8_e4m3fn_x4
+ALU = mybir.AluOpType
+ACT = mybir.ActivationFunctionType
+
+P = 128
+PACK = 4
+NF = P * PACK
+GRAPHS = 4
+PARTICLES = 64
+PAIRS = GRAPHS * PARTICLES
+HALVES = PAIRS // P
+GRAPHS_PER_HALF = GRAPHS // HALVES
+UNIT_SENDERS = 4
+UNITS_PER_HALF = PARTICLES // UNIT_SENDERS
+UNITS = HALVES * UNITS_PER_HALF
+UNIT_COLS = UNIT_SENDERS * P
+F_CHUNKS = NF // P
+WORDS = NF // 2
+X_BUFS = 12
+AHEAD = 2
+
+FLOPS = 2 * NF * NF * (GRAPHS * PARTICLES * PARTICLES + 4 * PAIRS)
+
+
+def tile_compositionalkoopmanoperators_pa_t_kernel(
+    tc, rel_enc, obj, rp_w, rp_b, pp_w, pp_b, out
+):
+    nc = tc.nc
+    with ExitStack() as stack:
+        stack.enter_context(tc.manual_schedule())
+        keep = stack.enter_context(tc.tile_pool(name="keep", bufs=1))
+        x_pool = stack.enter_context(tc.tile_pool(name="x_pool", bufs=X_BUFS))
+        q_pool = stack.enter_context(tc.tile_pool(name="q_pool", bufs=AHEAD + 1))
+        end_pool = stack.enter_context(tc.tile_pool(name="end_pool", bufs=2))
+        psum = stack.enter_context(tc.psum_pool(name="psum", bufs=4))
+
+        def mx_tiles(name, cols):
+            codes = keep.tile([P, cols], U32, name=name + "_codes", align_bytes=64)
+            scales = keep.tile([P, cols], U8, name=name + "_scales", align_bytes=64)
+            return codes, scales
+
+        def quantise(mx, grouped):
+            codes, scales = mx
+            nc.vector.quantize_mx(out=codes.bitcast(FP8X4), scales=scales, in_=grouped)
+
+        def mx_pass(bank, stationary, moving, start, stop):
+            nc.tensor.matmul_mx(
+                out=bank,
+                lhsT=stationary[0].bitcast(FP8X4),
+                lhsT_scale=stationary[1],
+                rhs=moving[0].bitcast(FP8X4),
+                rhs_scale=moving[1],
+                start=start,
+                stop=stop,
+            )
+
+        def columns(mx, first, count):
+            return mx[0][:, first : first + count], mx[1][:, first : first + count]
+
+        def load_weight(name, rows_by_partition):
+            raw = keep.tile([P, PACK * NF], BF16, name=name + "_raw")
+            a = rows_by_partition.shape[1]
+            nc.sync.dma_start(
+                out=raw[:].rearrange("p (a b) -> p a b", a=a), in_=rows_by_partition
+            )
+            return raw
+
+        def regroup_weight(name, raw, copy):
+            grouped = keep.tile([P, NF * PACK], BF16, name=name + "_grouped", align_bytes=64)
+            copy(
+                out=grouped[:].rearrange("p (n t) -> p n t", t=PACK),
+                in_=raw[:].rearrange("p (t n) -> p n t", t=PACK),
+            )
+            return grouped
+
+        def word_order(w):
+            return w.rearrange("(u q e) n -> q u (e n)", u=2, e=2)
+
+        def chunk_order(w):
+            return w.rearrange("(t p) n -> p t n", p=P)
+
+        rel_rows = rel_enc.rearrange("b i j k -> (b i) (j k)")
+        x_tiles = []
+
+        def load_unit(n):
+            half, quad = divmod(n, UNITS_PER_HALF)
+            x_sb = x_pool.tile([P, UNIT_SENDERS * NF], BF16, name="x_sb", tag="x_sb")
+            first = quad * UNIT_SENDERS * NF
+            nc.sync.dma_start(
+                out=x_sb[:],
+                in_=rel_rows[half * P : (half + 1) * P, first : first + UNIT_SENDERS * NF],
+            )
+            x_tiles.append(x_sb)
+
+        def transpose_words(bank, slot, words):
+            nc.tensor.transpose(bank[:, slot * P : (slot + 1) * P], words, ident[:])
+
+        grouped_units = []
+
+        def transpose_unit(n):
+            x_words = x_tiles[n][:].bitcast(F32)
+            grouped = q_pool.tile(
+                [P, UNIT_COLS * PACK], BF16, name="grouped", tag="grouped", align_bytes=64
+            )
+            grouped_words = grouped[:].bitcast(F32)
+            for pair in range(UNIT_SENDERS // 2):
+                bank = psum.tile([P, 4 * P], F32, name="flipped", tag="flipped")
+                for s in range(2):
+                    for u in range(2):
+                        first = (2 * pair + s) * WORDS + u * P
+                        transpose_words(bank, 2 * s + u, x_words[:, first : first + P])
+                nc.scalar.copy(
+                    out=grouped_words[:, pair * 4 * P : (pair + 1) * 4 * P].rearrange(
+                        "q (s c u) -> q s c u", s=2, u=2
+                    ),
+                    in_=bank[:].rearrange("q (s u c) -> q s c u", s=2, u=2),
+                )
+            grouped_units.append(grouped)
+
+        x_mx = []
+
+        def quantise_unit(n):
+            codes = q_pool.tile([P, UNIT_COLS], U32, name="x_codes", tag="x_codes", align_bytes=64)
+            scales = q_pool.tile(
+                [P, UNIT_COLS], U8, name="x_scales", tag="x_scales", align_bytes=64
+            )
+            quantise((codes[:], scales[:]), grouped_units[n][:])
+            x_mx.append((codes, scales))
+
+        def multiply_unit(n):
+            half, quad = divmod(n, UNITS_PER_HALF)
+            for c in range(F_CHUNKS):
+                bank = psum.tile([P, UNIT_COLS], F32, name="effect", tag="effect")
+                mx_pass(bank[:], columns(wr, c * P, P), columns(x_mx[n], 0, UNIT_COLS), True, False)
+                mx_pass(
+                    bank[:],
+                    columns(wi, c * P, P),
+                    columns(receivers, half * UNIT_COLS, UNIT_COLS),
+                    False,
+                    True,
+                )
+                for s in range(UNIT_SENDERS):
+                    for g in range(GRAPHS_PER_HALF):
+                        first = s * P + g * PARTICLES
+                        cols = slice(first, first + PARTICLES)
+                        sender = half * P + g * PARTICLES + quad * UNIT_SENDERS + s
+                        nc.vector.scalar_tensor_tensor(
+                            out=sums[half][:, c, cols],
+                            in0=bank[:, cols],
+                            scalar=neg_send[:, c, sender : sender + 1],
+                            in1=sums[half][:, c, cols],
+                            op0=ALU.max,
+                            op1=ALU.add,
+                        )
+
+        agg_mx = []
+
+        def quantise_agg(half):
+            joined = end_pool.tile([P, F_CHUNKS, 2 * P], F32, name="joined", tag="joined")
+            nc.vector.tensor_tensor(
+                out=joined[:],
+                in0=sums[half][:, :, 0 : 2 * P],
+                in1=sums[half][:, :, 2 * P : 4 * P],
+                op=ALU.add,
+            )
+            agg = end_pool.tile([P, P, PACK], BF16, name="agg", tag="agg", align_bytes=64)
+            for c in range(F_CHUNKS):
+                for g in range(GRAPHS_PER_HALF):
+                    graph = half * GRAPHS_PER_HALF + g
+                    first = g * PARTICLES
+                    nc.vector.scalar_tensor_tensor(
+                        out=agg[:, first : first + PARTICLES, c],
+                        in0=joined[:, c, first : first + PARTICLES],
+                        scalar=neg_send_sum[:, c * GRAPHS + graph : c * GRAPHS + graph + 1],
+                        in1=joined[:, c, P + first : P + first + PARTICLES],
+                        op0=ALU.subtract,
+                        op1=ALU.add,
+                    )
+            mx = mx_tiles("agg%d" % half, P)
+            quantise((mx[0][:], mx[1][:]), agg[:].rearrange("p c t -> p (c t)"))
+            agg_mx.append(mx)
+
+        def second_layer(half):
+            bank = psum.tile([P, NF], F32, name="particle", tag="effect")
+            mx_pass(bank[:], columns(receivers, half * UNIT_COLS, P), columns(po, 0, NF), True, False)
+            mx_pass(bank[:], columns(agg_mx[half], 0, P), columns(pa, 0, NF), False, True)
+            result = end_pool.tile([P, NF], F32, name="result", tag="result")
+            nc.vector.tensor_tensor(out=result[:], in0=bank[:], in1=pp_bias[:], op=ALU.add)
+            nc.scalar.activation(out=result[:], in_=result[:], func=ACT.Relu)
+            nc.sync.dma_start(out=out_rows[half * P : (half + 1) * P, :], in_=result[:])
+
+        out_rows = out.rearrange("b i n -> (b i) n")
+
+        bias_rows = keep.tile([P, P], BF16, name="bias_rows")
+        nc.vector.memset(bias_rows[:], 0.0)
+        sums = [keep.tile([P, F_CHUNKS, UNIT_COLS], F32, name="sums%d" % h) for h in range(HALVES)]
+        for half in range(HALVES):
+            nc.vector.memset(sums[half][:], 0.0)
+        ident = keep.tile([P, P], F32, name="ident")
+        make_identity(nc, ident[:])
+
+        obj_sb = keep.tile([P, HALVES * NF], BF16, name="obj_sb")
+        nc.sync.dma_start(
+            out=obj_sb[:].rearrange("p (h k) -> p h k", h=HALVES),
+            in_=obj.rearrange("b i k -> (b i) k").rearrange("(h p) k -> p h k", p=P),
+        )
+        nc.scalar.dma_start(out=bias_rows[0:F_CHUNKS, :], in_=rp_b.rearrange("(c p) -> c p", p=P))
+        wj_raw = load_weight("wj", word_order(rp_w[2 * NF : 3 * NF, :]))
+        load_unit(0)
+        wr_raw = load_weight("wr", word_order(rp_w[0:NF, :]))
+        wi_raw = load_weight("wi", word_order(rp_w[NF : 2 * NF, :]))
+        for n in range(1, X_BUFS):
+            load_unit(n)
+        po_raw = load_weight("po", word_order(pp_w[0:NF, :]))
+        pa_raw = load_weight("pa", chunk_order(pp_w[NF : 2 * NF, :]))
+        pp_bias = keep.tile([P, NF], BF16, name="pp_bias")
+        nc.sync.dma_start(out=pp_bias[:], in_=pp_b.partition_broadcast(P))
+
+        obj_words = obj_sb[:].bitcast(F32)
+        obj_bank = psum.tile([P, 4 * P], F32, name="obj_bank", tag="flipped")
+        for half in range(HALVES):
+            for u in range(2):
+                first = half * WORDS + u * P
+                transpose_words(obj_bank, 2 * half + u, obj_words[:, first : first + P])
+        receivers = mx_tiles("receivers", HALVES * UNIT_COLS)
+        repeated = []
+        for half in range(HALVES):
+            rep = keep.tile([P, UNIT_COLS * PACK], BF16, name="repeated%d" % half, align_bytes=64)
+            nc.vector.tensor_copy(
+                out=rep[:].bitcast(F32).rearrange("q (r c u) -> q r c u", r=UNIT_SENDERS, u=2),
+                in_=obj_bank[:, 2 * half * P : (2 * half + 2) * P]
+                .rearrange("q (u c) -> q c u", u=2)
+                .unsqueeze(1)
+                .to_broadcast([P, UNIT_SENDERS, P, 2]),
+            )
+            repeated.append(rep)
+
+        bias_f32 = keep.tile([P, P], F32, name="bias_f32")
+        nc.vector.tensor_copy(out=bias_f32[:], in_=bias_rows[:])
+        bias_bank = psum.tile([P, 4 * P], F32, name="bias_bank", tag="flipped")
+        transpose_words(bias_bank, 0, bias_f32[:])
+        rp_bias = keep.tile([P, F_CHUNKS], F32, name="rp_bias")
+
+        wj_grouped = regroup_weight("wj", wj_raw, nc.scalar.copy)
+        transpose_unit(0)
+        for half in range(HALVES):
+            quantise(columns(receivers, half * UNIT_COLS, UNIT_COLS), repeated[half][:])
+        nc.vector.tensor_copy(out=rp_bias[:], in_=bias_bank[:, 0:F_CHUNKS])
+        wr_grouped = regroup_weight("wr", wr_raw, nc.vector.tensor_copy)
+        wj = mx_tiles("wj", NF)
+        quantise((wj[0][:], wj[1][:]), wj_grouped[:])
+        wi_grouped = regroup_weight("wi", wi_raw, nc.vector.tensor_copy)
+        wr = mx_tiles("wr", NF)
+        quantise((wr[0][:], wr[1][:]), wr_grouped[:])
+        quantise_unit(0)
+        wi = mx_tiles("wi", NF)
+        quantise((wi[0][:], wi[1][:]), wi_grouped[:])
+
+        neg_send = keep.tile([P, F_CHUNKS, PAIRS], F32, name="neg_send")
+        for half in range(HALVES):
+            send_bank = psum.tile([P, F_CHUNKS * P], F32, name="send_bank", tag="effect")
+            for c in range(F_CHUNKS):
+                mx_pass(
+                    send_bank[:, c * P : (c + 1) * P],
+                    columns(wj, c * P, P),
+                    columns(receivers, half * UNIT_COLS, P),
+                    True,
+                    True,
+                )
+            for c in range(F_CHUNKS):
+                nc.vector.tensor_scalar(
+                    out=neg_send[:, c, half * P : (half + 1) * P],
+                    in0=send_bank[:, c * P : (c + 1) * P],
+                    scalar1=rp_bias[:, c : c + 1],
+                    scalar2=-1.0,
+                    op0=ALU.add,
+                    op1=ALU.mult,
+                )
+        neg_send_sum = keep.tile([P, F_CHUNKS * GRAPHS], F32, name="neg_send_sum")
+        nc.vector.tensor_reduce(
+            out=neg_send_sum[:],
+            in_=neg_send[:].rearrange("p c (b j) -> p (c b) j", j=PARTICLES),
+            axis=mybir.AxisListType.X,
+            op=ALU.add,
+        )
+
+        transpose_unit(1)
+        po_grouped = regroup_weight("po", po_raw, nc.scalar.copy)
+        pa_grouped = regroup_weight("pa", pa_raw, nc.scalar.copy)
+        po = mx_tiles("po", NF)
+        pa = mx_tiles("pa", NF)
+
+        for n in range(UNITS):
+            if n + AHEAD < UNITS:
+                transpose_unit(n + AHEAD)
+            if n + X_BUFS < UNITS:
+                load_unit(n + X_BUFS)
+            if n + 1 < UNITS:
+                quantise_unit(n + 1)
+            multiply_unit(n)
+            half, quad = divmod(n, UNITS_PER_HALF)
+            if half > 0 and quad == 0:
+                second_layer(half - 1)
+            if quad == UNITS_PER_HALF - 1:
+                if half == 0:
+                    quantise((po[0][:], po[1][:]), po_grouped[:])
+                    quantise((pa[0][:], pa[1][:]), pa_grouped[:])
+                quantise_agg(half)
+        second_layer(HALVES - 1)

@@ -16,19 +16,18 @@ PACK = 4
 NF = P * PACK
 GRAPHS = 4
 PARTICLES = 64
-PAIRS = GRAPHS * PARTICLES
-HALVES = PAIRS // P
-GRAPHS_PER_HALF = GRAPHS // HALVES
-UNIT_SENDERS = 4
-UNITS_PER_HALF = PARTICLES // UNIT_SENDERS
-UNITS = HALVES * UNITS_PER_HALF
-UNIT_COLS = UNIT_SENDERS * P
+HALF_GRAPHS = 2
+UNIT_COLS = 512
+UNIT_BLOCKS = UNIT_COLS // P
+UNIT_SLICES = UNIT_COLS // PARTICLES
+ROUNDS = HALF_GRAPHS * PARTICLES * PARTICLES // UNIT_COLS
 F_CHUNKS = NF // P
 WORDS = NF // 2
-X_BUFS = 12
+RUNNING = 2
+X_BUFS = 5
 AHEAD = 2
 
-FLOPS = 2 * NF * NF * (GRAPHS * PARTICLES * PARTICLES + 4 * PAIRS)
+FLOPS = 2 * NF * NF * (GRAPHS * PARTICLES * PARTICLES + 4 * GRAPHS * PARTICLES)
 
 
 def tile_compositionalkoopmanoperators_pa_t_kernel(
@@ -38,19 +37,24 @@ def tile_compositionalkoopmanoperators_pa_t_kernel(
     with ExitStack() as stack:
         stack.enter_context(tc.manual_schedule())
         keep = stack.enter_context(tc.tile_pool(name="keep", bufs=1))
-        x_pool = stack.enter_context(tc.tile_pool(name="x_pool", bufs=X_BUFS))
-        q_pool = stack.enter_context(tc.tile_pool(name="q_pool", bufs=AHEAD + 1))
+        x_pool = stack.enter_context(tc.tile_pool(name="x_pool", bufs=2 * X_BUFS))
+        q_pool = stack.enter_context(tc.tile_pool(name="q_pool", bufs=2 * (AHEAD + 1)))
         end_pool = stack.enter_context(tc.tile_pool(name="end_pool", bufs=2))
-        psum = stack.enter_context(tc.psum_pool(name="psum", bufs=4))
+        flip_psum = stack.enter_context(tc.psum_pool(name="flip_psum", bufs=4))
+        mx_psum = stack.enter_context(tc.psum_pool(name="mx_psum", bufs=2))
 
-        def mx_tiles(name, cols):
-            codes = keep.tile([P, cols], U32, name=name + "_codes", align_bytes=64)
-            scales = keep.tile([P, cols], U8, name=name + "_scales", align_bytes=64)
+        def mx_tiles(pool, name, cols):
+            codes = pool.tile([P, cols], U32, name=name + "_codes", tag=name + "_codes", align_bytes=64)
+            scales = pool.tile(
+                [P, cols], U8, name=name + "_scales", tag=name + "_scales", align_bytes=64
+            )
             return codes, scales
 
+        def columns(mx, first, count):
+            return mx[0][:, first : first + count], mx[1][:, first : first + count]
+
         def quantise(mx, grouped):
-            codes, scales = mx
-            nc.vector.quantize_mx(out=codes.bitcast(FP8X4), scales=scales, in_=grouped)
+            nc.vector.quantize_mx(out=mx[0].bitcast(FP8X4), scales=mx[1], in_=grouped)
 
         def mx_pass(bank, stationary, moving, start, stop):
             nc.tensor.matmul_mx(
@@ -62,9 +66,6 @@ def tile_compositionalkoopmanoperators_pa_t_kernel(
                 start=start,
                 stop=stop,
             )
-
-        def columns(mx, first, count):
-            return mx[0][:, first : first + count], mx[1][:, first : first + count]
 
         def load_weight(name, rows_by_partition):
             raw = keep.tile([P, PACK * NF], BF16, name=name + "_raw")
@@ -82,117 +83,121 @@ def tile_compositionalkoopmanoperators_pa_t_kernel(
             )
             return grouped
 
+        def quantise_weight(name, grouped):
+            mx = mx_tiles(keep, name, NF)
+            quantise(columns(mx, 0, NF), grouped[:])
+            return mx
+
         def word_order(w):
             return w.rearrange("(u q e) n -> q u (e n)", u=2, e=2)
 
         def chunk_order(w):
             return w.rearrange("(t p) n -> p t n", p=P)
 
-        rel_rows = rel_enc.rearrange("b i j k -> (b i) (j k)")
-        x_tiles = []
-
-        def load_unit(n):
-            half, quad = divmod(n, UNITS_PER_HALF)
-            x_sb = x_pool.tile([P, UNIT_SENDERS * NF], BF16, name="x_sb", tag="x_sb")
-            first = quad * UNIT_SENDERS * NF
-            nc.sync.dma_start(
-                out=x_sb[:],
-                in_=rel_rows[half * P : (half + 1) * P, first : first + UNIT_SENDERS * NF],
-            )
-            x_tiles.append(x_sb)
-
         def transpose_words(bank, slot, words):
             nc.tensor.transpose(bank[:, slot * P : (slot + 1) * P], words, ident[:])
 
-        grouped_units = []
+        by_pair = rel_enc.rearrange("b i j k -> (b i) (j k)")
+        by_relation = rel_enc.rearrange("b i j k -> (b i j) k")
+        x_rounds = []
 
-        def transpose_unit(n):
-            x_words = x_tiles[n][:].bitcast(F32)
+        def load_round(r):
+            x_sender = x_pool.tile([P, UNIT_BLOCKS * NF], BF16, name="x_sb", tag="x_sb")
+            first = r * UNIT_BLOCKS * NF
+            nc.sync.dma_start(out=x_sender[:], in_=by_pair[0:P, first : first + UNIT_BLOCKS * NF])
+            x_receiver = x_pool.tile([P, UNIT_BLOCKS * NF], BF16, name="x_sb", tag="x_sb")
+            first = (ROUNDS + r) * UNIT_COLS
+            nc.sync.dma_start(
+                out=x_receiver[:].rearrange("p (s k) -> p s k", s=UNIT_BLOCKS),
+                in_=by_relation[first : first + UNIT_COLS, :].rearrange("(s p) k -> p s k", p=P),
+            )
+            x_rounds.append((x_sender, x_receiver))
+
+        def transpose_unit(x_sb, copy):
+            x_words = x_sb[:].bitcast(F32)
             grouped = q_pool.tile(
                 [P, UNIT_COLS * PACK], BF16, name="grouped", tag="grouped", align_bytes=64
             )
             grouped_words = grouped[:].bitcast(F32)
-            for pair in range(UNIT_SENDERS // 2):
-                bank = psum.tile([P, 4 * P], F32, name="flipped", tag="flipped")
+            for pair in range(UNIT_BLOCKS // 2):
+                bank = flip_psum.tile([P, 4 * P], F32, name="flipped", tag="flipped")
                 for s in range(2):
                     for u in range(2):
                         first = (2 * pair + s) * WORDS + u * P
                         transpose_words(bank, 2 * s + u, x_words[:, first : first + P])
-                nc.scalar.copy(
+                copy(
                     out=grouped_words[:, pair * 4 * P : (pair + 1) * 4 * P].rearrange(
                         "q (s c u) -> q s c u", s=2, u=2
                     ),
                     in_=bank[:].rearrange("q (s u c) -> q s c u", s=2, u=2),
                 )
-            grouped_units.append(grouped)
+            return grouped
 
-        x_mx = []
+        grouped_rounds = []
 
-        def quantise_unit(n):
-            codes = q_pool.tile([P, UNIT_COLS], U32, name="x_codes", tag="x_codes", align_bytes=64)
-            scales = q_pool.tile(
-                [P, UNIT_COLS], U8, name="x_scales", tag="x_scales", align_bytes=64
-            )
-            quantise((codes[:], scales[:]), grouped_units[n][:])
-            x_mx.append((codes, scales))
-
-        def multiply_unit(n):
-            half, quad = divmod(n, UNITS_PER_HALF)
-            for c in range(F_CHUNKS):
-                bank = psum.tile([P, UNIT_COLS], F32, name="effect", tag="effect")
-                mx_pass(bank[:], columns(wr, c * P, P), columns(x_mx[n], 0, UNIT_COLS), True, False)
-                mx_pass(
-                    bank[:],
-                    columns(wi, c * P, P),
-                    columns(receivers, half * UNIT_COLS, UNIT_COLS),
-                    False,
-                    True,
+        def transpose_round(r):
+            grouped_rounds.append(
+                (
+                    transpose_unit(x_rounds[r][0], nc.vector.tensor_copy),
+                    transpose_unit(x_rounds[r][1], nc.scalar.copy),
                 )
-                for s in range(UNIT_SENDERS):
-                    for g in range(GRAPHS_PER_HALF):
-                        first = s * P + g * PARTICLES
-                        cols = slice(first, first + PARTICLES)
-                        sender = half * P + g * PARTICLES + quad * UNIT_SENDERS + s
+            )
+
+        mx_rounds = []
+
+        def quantise_round(r):
+            pair = []
+            for grouped in grouped_rounds[r]:
+                mx = mx_tiles(q_pool, "x", UNIT_COLS)
+                quantise(columns(mx, 0, UNIT_COLS), grouped[:])
+                pair.append(mx)
+            mx_rounds.append(pair)
+
+        def multiply_round(r):
+            graph = r * UNIT_SLICES // PARTICLES
+            for c in range(F_CHUNKS):
+                bank = mx_psum.tile([P, UNIT_COLS], F32, name="by_sender", tag="by_sender")
+                mx_pass(bank[:], columns(wr, c * P, P), columns(mx_rounds[r][0], 0, UNIT_COLS), True, False)
+                mx_pass(bank[:], columns(wi, c * P, P), columns(receivers, 0, UNIT_COLS), False, True)
+                for s in range(UNIT_BLOCKS):
+                    for g in range(HALF_GRAPHS):
+                        cols = slice(g * PARTICLES, (g + 1) * PARTICLES)
+                        sender = g * PARTICLES + r * UNIT_BLOCKS + s
                         nc.vector.scalar_tensor_tensor(
-                            out=sums[half][:, c, cols],
-                            in0=bank[:, cols],
+                            out=sums[:, c, s % RUNNING, cols],
+                            in0=bank[:, s * P + g * PARTICLES : s * P + (g + 1) * PARTICLES],
                             scalar=neg_send[:, c, sender : sender + 1],
-                            in1=sums[half][:, c, cols],
+                            in1=sums[:, c, s % RUNNING, cols],
                             op0=ALU.max,
                             op1=ALU.add,
                         )
 
-        agg_mx = []
-
-        def quantise_agg(half):
-            joined = end_pool.tile([P, F_CHUNKS, 2 * P], F32, name="joined", tag="joined")
-            nc.vector.tensor_tensor(
-                out=joined[:],
-                in0=sums[half][:, :, 0 : 2 * P],
-                in1=sums[half][:, :, 2 * P : 4 * P],
-                op=ALU.add,
-            )
-            agg = end_pool.tile([P, P, PACK], BF16, name="agg", tag="agg", align_bytes=64)
-            for c in range(F_CHUNKS):
-                for g in range(GRAPHS_PER_HALF):
-                    graph = half * GRAPHS_PER_HALF + g
-                    first = g * PARTICLES
-                    nc.vector.scalar_tensor_tensor(
-                        out=agg[:, first : first + PARTICLES, c],
-                        in0=joined[:, c, first : first + PARTICLES],
-                        scalar=neg_send_sum[:, c * GRAPHS + graph : c * GRAPHS + graph + 1],
-                        in1=joined[:, c, P + first : P + first + PARTICLES],
-                        op0=ALU.subtract,
-                        op1=ALU.add,
+                bank = mx_psum.tile([P, UNIT_COLS], F32, name="by_receiver", tag="by_receiver")
+                mx_pass(bank[:], columns(wr, c * P, P), columns(mx_rounds[r][1], 0, UNIT_COLS), True, False)
+                mx_pass(
+                    bank[:], columns(wj, c * P, P), columns(senders, graph * UNIT_COLS, UNIT_COLS), False, True
+                )
+                effects = end_pool.tile([P, UNIT_COLS], F32, name="effects", tag="effects")
+                for i in range(UNIT_SLICES):
+                    cols = slice(i * PARTICLES, (i + 1) * PARTICLES)
+                    receiver = r * UNIT_SLICES + i
+                    nc.scalar.activation(
+                        out=effects[:, cols],
+                        in_=bank[:, cols],
+                        func=ACT.Relu,
+                        bias=recv_bias[:, c, receiver : receiver + 1],
+                        accum_out=agg_receiver[:, c, receiver : receiver + 1],
                     )
-            mx = mx_tiles("agg%d" % half, P)
-            quantise((mx[0][:], mx[1][:]), agg[:].rearrange("p c t -> p (c t)"))
-            agg_mx.append(mx)
 
-        def second_layer(half):
-            bank = psum.tile([P, NF], F32, name="particle", tag="effect")
-            mx_pass(bank[:], columns(receivers, half * UNIT_COLS, P), columns(po, 0, NF), True, False)
-            mx_pass(bank[:], columns(agg_mx[half], 0, P), columns(pa, 0, NF), False, True)
+        def quantise_agg(name, agg):
+            agg_mx = mx_tiles(keep, name, P)
+            quantise(columns(agg_mx, 0, P), agg[:].rearrange("p c t -> p (c t)"))
+            return agg_mx
+
+        def second_layer(half, agg_mx):
+            bank = mx_psum.tile([P, NF], F32, name="particle", tag="by_sender")
+            mx_pass(bank[:], particles[half], columns(second["po"], 0, NF), True, False)
+            mx_pass(bank[:], columns(agg_mx, 0, P), columns(second["pa"], 0, NF), False, True)
             result = end_pool.tile([P, NF], F32, name="result", tag="result")
             nc.vector.tensor_tensor(out=result[:], in0=bank[:], in1=pp_bias[:], op=ALU.add)
             nc.scalar.activation(out=result[:], in_=result[:], func=ACT.Relu)
@@ -202,117 +207,144 @@ def tile_compositionalkoopmanoperators_pa_t_kernel(
 
         bias_rows = keep.tile([P, P], BF16, name="bias_rows")
         nc.vector.memset(bias_rows[:], 0.0)
-        sums = [keep.tile([P, F_CHUNKS, UNIT_COLS], F32, name="sums%d" % h) for h in range(HALVES)]
-        for half in range(HALVES):
-            nc.vector.memset(sums[half][:], 0.0)
+        sums = keep.tile([P, F_CHUNKS, RUNNING, P], F32, name="sums")
+        nc.vector.memset(sums[:], 0.0)
         ident = keep.tile([P, P], F32, name="ident")
         make_identity(nc, ident[:])
 
-        obj_sb = keep.tile([P, HALVES * NF], BF16, name="obj_sb")
+        obj_sb = keep.tile([P, 2 * NF], BF16, name="obj_sb")
         nc.sync.dma_start(
-            out=obj_sb[:].rearrange("p (h k) -> p h k", h=HALVES),
+            out=obj_sb[:].rearrange("p (h k) -> p h k", h=2),
             in_=obj.rearrange("b i k -> (b i) k").rearrange("(h p) k -> p h k", p=P),
         )
         nc.scalar.dma_start(out=bias_rows[0:F_CHUNKS, :], in_=rp_b.rearrange("(c p) -> c p", p=P))
-        wj_raw = load_weight("wj", word_order(rp_w[2 * NF : 3 * NF, :]))
-        load_unit(0)
-        wr_raw = load_weight("wr", word_order(rp_w[0:NF, :]))
         wi_raw = load_weight("wi", word_order(rp_w[NF : 2 * NF, :]))
-        for n in range(1, X_BUFS):
-            load_unit(n)
-        po_raw = load_weight("po", word_order(pp_w[0:NF, :]))
-        pa_raw = load_weight("pa", chunk_order(pp_w[NF : 2 * NF, :]))
+        wj_raw = load_weight("wj", word_order(rp_w[2 * NF : 3 * NF, :]))
+        wr_raw = load_weight("wr", word_order(rp_w[0:NF, :]))
+        for r in range(X_BUFS):
+            load_round(r)
+        second_raw = [
+            ("po", load_weight("po", word_order(pp_w[0:NF, :]))),
+            ("pa", load_weight("pa", chunk_order(pp_w[NF : 2 * NF, :]))),
+        ]
         pp_bias = keep.tile([P, NF], BF16, name="pp_bias")
         nc.sync.dma_start(out=pp_bias[:], in_=pp_b.partition_broadcast(P))
 
         obj_words = obj_sb[:].bitcast(F32)
-        obj_bank = psum.tile([P, 4 * P], F32, name="obj_bank", tag="flipped")
-        for half in range(HALVES):
+        obj_banks = []
+        for half in range(2):
+            obj_bank = flip_psum.tile([P, 4 * P], F32, name="obj_bank", tag="flipped")
             for u in range(2):
                 first = half * WORDS + u * P
-                transpose_words(obj_bank, 2 * half + u, obj_words[:, first : first + P])
-        receivers = mx_tiles("receivers", HALVES * UNIT_COLS)
-        repeated = []
-        for half in range(HALVES):
-            rep = keep.tile([P, UNIT_COLS * PACK], BF16, name="repeated%d" % half, align_bytes=64)
-            nc.vector.tensor_copy(
-                out=rep[:].bitcast(F32).rearrange("q (r c u) -> q r c u", r=UNIT_SENDERS, u=2),
-                in_=obj_bank[:, 2 * half * P : (2 * half + 2) * P]
-                .rearrange("q (u c) -> q c u", u=2)
+                transpose_words(obj_bank, u, obj_words[:, first : first + P])
+            obj_banks.append(obj_bank)
+
+        def repeat(name, first, count, copy):
+            half, col = divmod(first, P)
+            times = UNIT_COLS // count
+            rep = keep.tile([P, UNIT_COLS * PACK], BF16, name=name, align_bytes=64)
+            copy(
+                out=rep[:].bitcast(F32).rearrange("q (r c u) -> q r c u", r=times, u=2),
+                in_=obj_banks[half][:, 0 : 2 * P]
+                .rearrange("q (u c) -> q c u", u=2)[:, col : col + count, :]
                 .unsqueeze(1)
-                .to_broadcast([P, UNIT_SENDERS, P, 2]),
+                .to_broadcast([P, times, count, 2]),
             )
-            repeated.append(rep)
+            return rep
+
+        receivers_rep = repeat("receivers_rep", 0, P, nc.vector.tensor_copy)
+        senders_rep = [
+            repeat("senders_rep%d" % g, P + g * PARTICLES, PARTICLES, nc.scalar.copy)
+            for g in range(HALF_GRAPHS)
+        ]
+        receivers = mx_tiles(keep, "receivers", UNIT_COLS)
+        senders = mx_tiles(keep, "senders", HALF_GRAPHS * UNIT_COLS)
 
         bias_f32 = keep.tile([P, P], F32, name="bias_f32")
         nc.vector.tensor_copy(out=bias_f32[:], in_=bias_rows[:])
-        bias_bank = psum.tile([P, 4 * P], F32, name="bias_bank", tag="flipped")
+        bias_bank = flip_psum.tile([P, 4 * P], F32, name="bias_bank", tag="flipped")
         transpose_words(bias_bank, 0, bias_f32[:])
         rp_bias = keep.tile([P, F_CHUNKS], F32, name="rp_bias")
 
+        quantise(columns(receivers, 0, UNIT_COLS), receivers_rep[:])
+        wi_grouped = regroup_weight("wi", wi_raw, nc.vector.tensor_copy)
         wj_grouped = regroup_weight("wj", wj_raw, nc.scalar.copy)
-        transpose_unit(0)
-        for half in range(HALVES):
-            quantise(columns(receivers, half * UNIT_COLS, UNIT_COLS), repeated[half][:])
+        for g in range(HALF_GRAPHS):
+            quantise(columns(senders, g * UNIT_COLS, UNIT_COLS), senders_rep[g][:])
         nc.vector.tensor_copy(out=rp_bias[:], in_=bias_bank[:, 0:F_CHUNKS])
         wr_grouped = regroup_weight("wr", wr_raw, nc.vector.tensor_copy)
-        wj = mx_tiles("wj", NF)
-        quantise((wj[0][:], wj[1][:]), wj_grouped[:])
-        wi_grouped = regroup_weight("wi", wi_raw, nc.vector.tensor_copy)
-        wr = mx_tiles("wr", NF)
-        quantise((wr[0][:], wr[1][:]), wr_grouped[:])
-        quantise_unit(0)
-        wi = mx_tiles("wi", NF)
-        quantise((wi[0][:], wi[1][:]), wi_grouped[:])
+        wi = quantise_weight("wi", wi_grouped)
+        wj = quantise_weight("wj", wj_grouped)
+        transpose_round(0)
+        wr = quantise_weight("wr", wr_grouped)
 
-        neg_send = keep.tile([P, F_CHUNKS, PAIRS], F32, name="neg_send")
-        for half in range(HALVES):
-            send_bank = psum.tile([P, F_CHUNKS * P], F32, name="send_bank", tag="effect")
-            for c in range(F_CHUNKS):
-                mx_pass(
-                    send_bank[:, c * P : (c + 1) * P],
-                    columns(wj, c * P, P),
-                    columns(receivers, half * UNIT_COLS, P),
-                    True,
-                    True,
-                )
-            for c in range(F_CHUNKS):
-                nc.vector.tensor_scalar(
-                    out=neg_send[:, c, half * P : (half + 1) * P],
-                    in0=send_bank[:, c * P : (c + 1) * P],
-                    scalar1=rp_bias[:, c : c + 1],
-                    scalar2=-1.0,
-                    op0=ALU.add,
-                    op1=ALU.mult,
-                )
-        neg_send_sum = keep.tile([P, F_CHUNKS * GRAPHS], F32, name="neg_send_sum")
+        particles = (
+            columns(receivers, 0, P),
+            columns(senders, UNIT_COLS - PARTICLES, P),
+        )
+
+        neg_send = keep.tile([P, F_CHUNKS, P], F32, name="neg_send")
+        recv_bias = keep.tile([P, F_CHUNKS, P], F32, name="recv_bias")
+        send_bank = mx_psum.tile([P, F_CHUNKS * P], F32, name="send_bank", tag="by_sender")
+        recv_bank = mx_psum.tile([P, F_CHUNKS * P], F32, name="recv_bank", tag="by_receiver")
+        for c in range(F_CHUNKS):
+            mx_pass(send_bank[:, c * P : (c + 1) * P], columns(wj, c * P, P), particles[0], True, True)
+        for c in range(F_CHUNKS):
+            mx_pass(recv_bank[:, c * P : (c + 1) * P], columns(wi, c * P, P), particles[1], True, True)
+        for c in range(F_CHUNKS):
+            nc.vector.tensor_scalar(
+                out=neg_send[:, c, :],
+                in0=send_bank[:, c * P : (c + 1) * P],
+                scalar1=rp_bias[:, c : c + 1],
+                scalar2=-1.0,
+                op0=ALU.add,
+                op1=ALU.mult,
+            )
+            nc.scalar.activation(
+                out=recv_bias[:, c, :],
+                in_=recv_bank[:, c * P : (c + 1) * P],
+                func=ACT.Identity,
+                bias=rp_bias[:, c : c + 1],
+            )
+        quantise_round(0)
+        neg_send_sum = keep.tile([P, F_CHUNKS * HALF_GRAPHS], F32, name="neg_send_sum")
         nc.vector.tensor_reduce(
             out=neg_send_sum[:],
             in_=neg_send[:].rearrange("p c (b j) -> p (c b) j", j=PARTICLES),
             axis=mybir.AxisListType.X,
             op=ALU.add,
         )
+        agg_receiver = keep.tile([P, F_CHUNKS, P], F32, name="agg_receiver")
+        transpose_round(1)
 
-        transpose_unit(1)
-        po_grouped = regroup_weight("po", po_raw, nc.scalar.copy)
-        pa_grouped = regroup_weight("pa", pa_raw, nc.scalar.copy)
-        po = mx_tiles("po", NF)
-        pa = mx_tiles("pa", NF)
+        second = {}
+        for r in range(ROUNDS):
+            if r + 1 < ROUNDS:
+                quantise_round(r + 1)
+            if r + AHEAD < ROUNDS:
+                transpose_round(r + AHEAD)
+            if r + X_BUFS < ROUNDS:
+                load_round(r + X_BUFS)
+            multiply_round(r)
+            if r < len(second_raw):
+                name, raw = second_raw[r]
+                second[name] = quantise_weight(name, regroup_weight(name, raw, nc.vector.tensor_copy))
 
-        for n in range(UNITS):
-            if n + AHEAD < UNITS:
-                transpose_unit(n + AHEAD)
-            if n + X_BUFS < UNITS:
-                load_unit(n + X_BUFS)
-            if n + 1 < UNITS:
-                quantise_unit(n + 1)
-            multiply_unit(n)
-            half, quad = divmod(n, UNITS_PER_HALF)
-            if half > 0 and quad == 0:
-                second_layer(half - 1)
-            if quad == UNITS_PER_HALF - 1:
-                if half == 0:
-                    quantise((po[0][:], po[1][:]), po_grouped[:])
-                    quantise((pa[0][:], pa[1][:]), pa_grouped[:])
-                quantise_agg(half)
-        second_layer(HALVES - 1)
+        agg_by_receiver = end_pool.tile([P, P, PACK], BF16, name="agg_r", tag="agg_r", align_bytes=64)
+        nc.scalar.copy(out=agg_by_receiver[:], in_=agg_receiver[:].rearrange("p c n -> p n c"))
+        agg_by_sender = end_pool.tile([P, P, PACK], BF16, name="agg_s", tag="agg_s", align_bytes=64)
+        for c in range(F_CHUNKS):
+            for g in range(HALF_GRAPHS):
+                cols = slice(g * PARTICLES, (g + 1) * PARTICLES)
+                nc.vector.scalar_tensor_tensor(
+                    out=agg_by_sender[:, cols, c],
+                    in0=sums[:, c, 0, cols],
+                    scalar=neg_send_sum[:, c * HALF_GRAPHS + g : c * HALF_GRAPHS + g + 1],
+                    in1=sums[:, c, 1, cols],
+                    op0=ALU.subtract,
+                    op1=ALU.add,
+                )
+        agg_mx_receiver = quantise_agg("agg_r", agg_by_receiver)
+        agg_mx_sender = quantise_agg("agg_s", agg_by_sender)
+        second_layer(1, agg_mx_receiver)
+        second_layer(0, agg_mx_sender)

@@ -38,7 +38,7 @@ def tile_compositionalkoopmanoperators_pa_t_kernel(
         stack.enter_context(tc.manual_schedule())
         keep = stack.enter_context(tc.tile_pool(name="keep", bufs=1))
         x_pool = stack.enter_context(tc.tile_pool(name="x_pool", bufs=2 * X_BUFS))
-        q_pool = stack.enter_context(tc.tile_pool(name="q_pool", bufs=2 * (AHEAD + 1)))
+        q_pool = stack.enter_context(tc.tile_pool(name="q_pool", bufs=2 * AHEAD))
         end_pool = stack.enter_context(tc.tile_pool(name="end_pool", bufs=2))
         flip_psum = stack.enter_context(tc.psum_pool(name="flip_psum", bufs=4))
         mx_psum = stack.enter_context(tc.psum_pool(name="mx_psum", bufs=2))
@@ -75,13 +75,18 @@ def tile_compositionalkoopmanoperators_pa_t_kernel(
             )
             return raw
 
-        def regroup_weight(name, raw, copy):
-            grouped = keep.tile([P, NF * PACK], BF16, name=name + "_grouped", align_bytes=64)
+        def grouped_tile(name):
+            return keep.tile([P, NF * PACK], BF16, name=name + "_grouped", align_bytes=64)
+
+        def regroup_weight(grouped, raw, first, count, copy):
             copy(
-                out=grouped[:].rearrange("p (n t) -> p n t", t=PACK),
-                in_=raw[:].rearrange("p (t n) -> p n t", t=PACK),
+                out=grouped[:, first * PACK : (first + count) * PACK].rearrange(
+                    "p (c i t) -> p c t i", i=4, t=PACK
+                ),
+                in_=raw[:]
+                .rearrange("p (t n) -> p t n", t=PACK)[:, :, first : first + count]
+                .rearrange("p t (c i) -> p c t i", i=4),
             )
-            return grouped
 
         def quantise_weight(name, grouped):
             mx = mx_tiles(keep, name, NF)
@@ -146,16 +151,16 @@ def tile_compositionalkoopmanoperators_pa_t_kernel(
         mx_rounds = []
 
         def quantise_round(r):
-            pair = []
-            for grouped in grouped_rounds[r]:
-                mx = mx_tiles(q_pool, "x", UNIT_COLS)
-                quantise(columns(mx, 0, UNIT_COLS), grouped[:])
-                pair.append(mx)
+            pair = [mx_tiles(q_pool, "x", UNIT_COLS) for kind in range(2)]
+            for kind in (1, 0):
+                quantise(columns(pair[kind], 0, UNIT_COLS), grouped_rounds[r][kind][:])
             mx_rounds.append(pair)
 
         def multiply_round(r):
             graph = r * UNIT_SLICES // PARTICLES
             for c in range(F_CHUNKS):
+                if c == F_CHUNKS // 2 and r + 1 < ROUNDS:
+                    quantise_round(r + 1)
                 bank = mx_psum.tile([P, UNIT_COLS], F32, name="by_sender", tag="by_sender")
                 mx_pass(bank[:], columns(wr, c * P, P), columns(mx_rounds[r][0], 0, UNIT_COLS), True, False)
                 mx_pass(bank[:], columns(wi, c * P, P), columns(receivers, 0, UNIT_COLS), False, True)
@@ -189,20 +194,6 @@ def tile_compositionalkoopmanoperators_pa_t_kernel(
                         accum_out=agg_receiver[:, c, receiver : receiver + 1],
                     )
 
-        def quantise_agg(name, agg):
-            agg_mx = mx_tiles(keep, name, P)
-            quantise(columns(agg_mx, 0, P), agg[:].rearrange("p c t -> p (c t)"))
-            return agg_mx
-
-        def second_layer(half, agg_mx):
-            bank = mx_psum.tile([P, NF], F32, name="particle", tag="by_sender")
-            mx_pass(bank[:], particles[half], columns(second["po"], 0, NF), True, False)
-            mx_pass(bank[:], columns(agg_mx, 0, P), columns(second["pa"], 0, NF), False, True)
-            result = end_pool.tile([P, NF], F32, name="result", tag="result")
-            nc.vector.tensor_tensor(out=result[:], in0=bank[:], in1=pp_bias[:], op=ALU.add)
-            nc.scalar.activation(out=result[:], in_=result[:], func=ACT.Relu)
-            nc.sync.dma_start(out=out_rows[half * P : (half + 1) * P, :], in_=result[:])
-
         out_rows = out.rearrange("b i n -> (b i) n")
 
         bias_rows = keep.tile([P, P], BF16, name="bias_rows")
@@ -219,31 +210,29 @@ def tile_compositionalkoopmanoperators_pa_t_kernel(
         )
         nc.scalar.dma_start(out=bias_rows[0:F_CHUNKS, :], in_=rp_b.rearrange("(c p) -> c p", p=P))
         wi_raw = load_weight("wi", word_order(rp_w[NF : 2 * NF, :]))
-        wj_raw = load_weight("wj", word_order(rp_w[2 * NF : 3 * NF, :]))
         wr_raw = load_weight("wr", word_order(rp_w[0:NF, :]))
+        wj_raw = load_weight("wj", word_order(rp_w[2 * NF : 3 * NF, :]))
         for r in range(X_BUFS):
             load_round(r)
-        second_raw = [
-            ("po", load_weight("po", word_order(pp_w[0:NF, :]))),
-            ("pa", load_weight("pa", chunk_order(pp_w[NF : 2 * NF, :]))),
-        ]
+        po_raw = load_weight("po", word_order(pp_w[0:NF, :]))
+        pa_raw = load_weight("pa", chunk_order(pp_w[NF : 2 * NF, :]))
         pp_bias = keep.tile([P, NF], BF16, name="pp_bias")
         nc.sync.dma_start(out=pp_bias[:], in_=pp_b.partition_broadcast(P))
 
         obj_words = obj_sb[:].bitcast(F32)
         obj_banks = []
-        for half in range(2):
-            obj_bank = flip_psum.tile([P, 4 * P], F32, name="obj_bank", tag="flipped")
+        for half, tag in enumerate(("by_sender", "by_receiver")):
+            obj_bank = mx_psum.tile([P, 4 * P], F32, name="obj_bank", tag=tag)
             for u in range(2):
                 first = half * WORDS + u * P
                 transpose_words(obj_bank, u, obj_words[:, first : first + P])
             obj_banks.append(obj_bank)
 
-        def repeat(name, first, count, copy):
+        def repeat(name, first, count):
             half, col = divmod(first, P)
             times = UNIT_COLS // count
             rep = keep.tile([P, UNIT_COLS * PACK], BF16, name=name, align_bytes=64)
-            copy(
+            nc.scalar.copy(
                 out=rep[:].bitcast(F32).rearrange("q (r c u) -> q r c u", r=times, u=2),
                 in_=obj_banks[half][:, 0 : 2 * P]
                 .rearrange("q (u c) -> q c u", u=2)[:, col : col + count, :]
@@ -252,31 +241,33 @@ def tile_compositionalkoopmanoperators_pa_t_kernel(
             )
             return rep
 
-        receivers_rep = repeat("receivers_rep", 0, P, nc.vector.tensor_copy)
+        receivers_rep = repeat("receivers_rep", 0, P)
         senders_rep = [
-            repeat("senders_rep%d" % g, P + g * PARTICLES, PARTICLES, nc.scalar.copy)
-            for g in range(HALF_GRAPHS)
+            repeat("senders_rep%d" % g, P + g * PARTICLES, PARTICLES) for g in range(HALF_GRAPHS)
         ]
         receivers = mx_tiles(keep, "receivers", UNIT_COLS)
         senders = mx_tiles(keep, "senders", HALF_GRAPHS * UNIT_COLS)
 
         bias_f32 = keep.tile([P, P], F32, name="bias_f32")
         nc.vector.tensor_copy(out=bias_f32[:], in_=bias_rows[:])
-        bias_bank = flip_psum.tile([P, 4 * P], F32, name="bias_bank", tag="flipped")
+        bias_bank = mx_psum.tile([P, 4 * P], F32, name="bias_bank", tag="by_sender")
         transpose_words(bias_bank, 0, bias_f32[:])
         rp_bias = keep.tile([P, F_CHUNKS], F32, name="rp_bias")
 
+        wi_grouped, wr_grouped, wj_grouped = grouped_tile("wi"), grouped_tile("wr"), grouped_tile("wj")
+        regroup_weight(wi_grouped, wi_raw, 0, NF, nc.vector.tensor_copy)
         quantise(columns(receivers, 0, UNIT_COLS), receivers_rep[:])
-        wi_grouped = regroup_weight("wi", wi_raw, nc.vector.tensor_copy)
-        wj_grouped = regroup_weight("wj", wj_raw, nc.scalar.copy)
+        regroup_weight(wr_grouped, wr_raw, 0, NF, nc.vector.tensor_copy)
+        regroup_weight(wj_grouped, wj_raw, 0, NF, nc.scalar.copy)
+        nc.vector.tensor_copy(out=rp_bias[:], in_=bias_bank[:, 0:F_CHUNKS])
         for g in range(HALF_GRAPHS):
             quantise(columns(senders, g * UNIT_COLS, UNIT_COLS), senders_rep[g][:])
-        nc.vector.tensor_copy(out=rp_bias[:], in_=bias_bank[:, 0:F_CHUNKS])
-        wr_grouped = regroup_weight("wr", wr_raw, nc.vector.tensor_copy)
         wi = quantise_weight("wi", wi_grouped)
-        wj = quantise_weight("wj", wj_grouped)
-        transpose_round(0)
         wr = quantise_weight("wr", wr_grouped)
+        transpose_round(0)
+        wj = quantise_weight("wj", wj_grouped)
+        quantise_round(0)
+        transpose_round(1)
 
         particles = (
             columns(receivers, 0, P),
@@ -306,45 +297,69 @@ def tile_compositionalkoopmanoperators_pa_t_kernel(
                 func=ACT.Identity,
                 bias=rp_bias[:, c : c + 1],
             )
-        quantise_round(0)
-        neg_send_sum = keep.tile([P, F_CHUNKS * HALF_GRAPHS], F32, name="neg_send_sum")
-        nc.vector.tensor_reduce(
-            out=neg_send_sum[:],
-            in_=neg_send[:].rearrange("p c (b j) -> p (c b) j", j=PARTICLES),
-            axis=mybir.AxisListType.X,
-            op=ALU.add,
-        )
         agg_receiver = keep.tile([P, F_CHUNKS, P], F32, name="agg_receiver")
-        transpose_round(1)
 
+        neg_send_sum = keep.tile([P, F_CHUNKS * HALF_GRAPHS], F32, name="neg_send_sum")
         second = {}
+
+        def sum_neg_send():
+            nc.vector.tensor_reduce(
+                out=neg_send_sum[:],
+                in_=neg_send[:].rearrange("p c (b j) -> p (c b) j", j=PARTICLES),
+                axis=mybir.AxisListType.X,
+                op=ALU.add,
+            )
+
+        def quantise_second(name, grouped):
+            second[name] = quantise_weight(name, grouped)
+
+        chores = [sum_neg_send]
+        for name, raw in (("po", po_raw), ("pa", pa_raw)):
+            grouped = grouped_tile(name)
+            for c in range(F_CHUNKS):
+                chores.append(
+                    lambda grouped=grouped, raw=raw, c=c: regroup_weight(
+                        grouped, raw, c * P, P, nc.scalar.copy
+                    )
+                )
+            chores.append(lambda name=name, grouped=grouped: quantise_second(name, grouped))
+
         for r in range(ROUNDS):
-            if r + 1 < ROUNDS:
-                quantise_round(r + 1)
+            multiply_round(r)
             if r + AHEAD < ROUNDS:
                 transpose_round(r + AHEAD)
             if r + X_BUFS < ROUNDS:
                 load_round(r + X_BUFS)
-            multiply_round(r)
-            if r < len(second_raw):
-                name, raw = second_raw[r]
-                second[name] = quantise_weight(name, regroup_weight(name, raw, nc.vector.tensor_copy))
+            if r < len(chores):
+                chores[r]()
 
-        agg_by_receiver = end_pool.tile([P, P, PACK], BF16, name="agg_r", tag="agg_r", align_bytes=64)
-        nc.scalar.copy(out=agg_by_receiver[:], in_=agg_receiver[:].rearrange("p c n -> p n c"))
-        agg_by_sender = end_pool.tile([P, P, PACK], BF16, name="agg_s", tag="agg_s", align_bytes=64)
+        banks = []
+        for half in range(2):
+            bank = flip_psum.tile([P, NF], F32, name="particle", tag="flipped")
+            mx_pass(bank[:], particles[half], columns(second["po"], 0, NF), True, False)
+            banks.append(bank)
+        agg = [
+            end_pool.tile([P, P, PACK], BF16, name="agg%d" % half, tag="agg%d" % half, align_bytes=64)
+            for half in range(2)
+        ]
+        nc.scalar.copy(out=agg[1][:], in_=agg_receiver[:].rearrange("p c n -> p n c"))
         for c in range(F_CHUNKS):
             for g in range(HALF_GRAPHS):
                 cols = slice(g * PARTICLES, (g + 1) * PARTICLES)
                 nc.vector.scalar_tensor_tensor(
-                    out=agg_by_sender[:, cols, c],
+                    out=agg[0][:, cols, c],
                     in0=sums[:, c, 0, cols],
                     scalar=neg_send_sum[:, c * HALF_GRAPHS + g : c * HALF_GRAPHS + g + 1],
                     in1=sums[:, c, 1, cols],
                     op0=ALU.subtract,
                     op1=ALU.add,
                 )
-        agg_mx_receiver = quantise_agg("agg_r", agg_by_receiver)
-        agg_mx_sender = quantise_agg("agg_s", agg_by_sender)
-        second_layer(1, agg_mx_receiver)
-        second_layer(0, agg_mx_sender)
+        agg_mx = [mx_tiles(keep, "agg%d" % half, P) for half in range(2)]
+        for half in (1, 0):
+            quantise(columns(agg_mx[half], 0, P), agg[half][:].rearrange("p c t -> p (c t)"))
+        for half in (1, 0):
+            mx_pass(banks[half][:], columns(agg_mx[half], 0, P), columns(second["pa"], 0, NF), False, True)
+            result = end_pool.tile([P, NF], F32, name="result", tag="result")
+            nc.vector.tensor_tensor(out=result[:], in0=banks[half][:], in1=pp_bias[:], op=ALU.add)
+            nc.scalar.activation(out=result[:], in_=result[:], func=ACT.Relu)
+            nc.sync.dma_start(out=out_rows[half * P : (half + 1) * P, :], in_=result[:])

@@ -24,6 +24,7 @@ ROUNDS = HALF_GRAPHS * PARTICLES * PARTICLES // UNIT_COLS
 F_CHUNKS = NF // P
 WORDS = NF // 2
 RUNNING = 2
+POOL_CHUNKS = 2
 X_BUFS = 5
 AHEAD = 2
 
@@ -162,20 +163,39 @@ def tile_compositionalkoopmanoperators_pa_t_kernel(
                 if c == F_CHUNKS // 2 and r + 1 < ROUNDS:
                     quantise_round(r + 1)
                 bank = mx_psum.tile([P, UNIT_COLS], F32, name="by_sender", tag="by_sender")
-                mx_pass(bank[:], columns(wr, c * P, P), columns(mx_rounds[r][0], 0, UNIT_COLS), True, False)
-                mx_pass(bank[:], columns(wi, c * P, P), columns(receivers, 0, UNIT_COLS), False, True)
+                by_pool = c < POOL_CHUNKS
+                mx_pass(bank[:], columns(wr, c * P, P), columns(mx_rounds[r][0], 0, UNIT_COLS), True, by_pool)
+                if by_pool:
+                    clipped = end_pool.tile([P, UNIT_COLS], F32, name="clipped", tag="clipped", bufs=3)
+                else:
+                    mx_pass(bank[:], columns(wi, c * P, P), columns(receivers, 0, UNIT_COLS), False, True)
                 for s in range(UNIT_BLOCKS):
                     for g in range(HALF_GRAPHS):
                         cols = slice(g * PARTICLES, (g + 1) * PARTICLES)
+                        bank_cols = slice(s * P + g * PARTICLES, s * P + (g + 1) * PARTICLES)
                         sender = g * PARTICLES + r * UNIT_BLOCKS + s
-                        nc.vector.scalar_tensor_tensor(
-                            out=sums[:, c, s % RUNNING, cols],
-                            in0=bank[:, s * P + g * PARTICLES : s * P + (g + 1) * PARTICLES],
-                            scalar=neg_send[:, c, sender : sender + 1],
-                            in1=sums[:, c, s % RUNNING, cols],
-                            op0=ALU.max,
-                            op1=ALU.add,
-                        )
+                        if by_pool:
+                            nc.vector.scalar_tensor_tensor(
+                                out=clipped[:, bank_cols],
+                                in0=bank[:, bank_cols],
+                                scalar=send_term[:, c, sender : sender + 1],
+                                in1=neg_recv[:, c, cols],
+                                op0=ALU.add,
+                                op1=ALU.max,
+                            )
+                        else:
+                            nc.vector.scalar_tensor_tensor(
+                                out=sums[:, c, s % RUNNING, cols],
+                                in0=bank[:, bank_cols],
+                                scalar=send_term[:, c, sender : sender + 1],
+                                in1=sums[:, c, s % RUNNING, cols],
+                                op0=ALU.max,
+                                op1=ALU.add,
+                            )
+                if by_pool:
+                    nc.gpsimd.tensor_tensor(
+                        out=pool_sums[:, c, :], in0=pool_sums[:, c, :], in1=clipped[:], op=ALU.add
+                    )
 
                 bank = mx_psum.tile([P, UNIT_COLS], F32, name="by_receiver", tag="by_receiver")
                 mx_pass(bank[:], columns(wr, c * P, P), columns(mx_rounds[r][1], 0, UNIT_COLS), True, False)
@@ -274,7 +294,9 @@ def tile_compositionalkoopmanoperators_pa_t_kernel(
             columns(senders, UNIT_COLS - PARTICLES, P),
         )
 
-        neg_send = keep.tile([P, F_CHUNKS, P], F32, name="neg_send")
+        send_term = keep.tile([P, F_CHUNKS, P], F32, name="send_term")
+        neg_recv = keep.tile([P, POOL_CHUNKS, P], F32, name="neg_recv")
+        pool_sums = keep.tile([P, POOL_CHUNKS, UNIT_COLS], F32, name="pool_sums")
         recv_bias = keep.tile([P, F_CHUNKS, P], F32, name="recv_bias")
         send_bank = mx_psum.tile([P, F_CHUNKS * P], F32, name="send_bank", tag="by_sender")
         recv_bank = mx_psum.tile([P, F_CHUNKS * P], F32, name="recv_bank", tag="by_receiver")
@@ -282,12 +304,23 @@ def tile_compositionalkoopmanoperators_pa_t_kernel(
             mx_pass(send_bank[:, c * P : (c + 1) * P], columns(wj, c * P, P), particles[0], True, True)
         for c in range(F_CHUNKS):
             mx_pass(recv_bank[:, c * P : (c + 1) * P], columns(wi, c * P, P), particles[1], True, True)
+        own_bank = flip_psum.tile([P, 4 * P], F32, name="own_bank", tag="flipped")
+        for c in range(POOL_CHUNKS):
+            mx_pass(own_bank[:, c * P : (c + 1) * P], columns(wi, c * P, P), particles[0], True, True)
+        nc.vector.memset(pool_sums[:, :, P:UNIT_COLS], 0.0)
+        for c in range(POOL_CHUNKS):
+            nc.vector.tensor_scalar_mul(
+                out=neg_recv[:, c, :], in0=own_bank[:, c * P : (c + 1) * P], scalar1=-1.0
+            )
+            nc.vector.tensor_scalar_mul(
+                out=pool_sums[:, c, 0:P], in0=own_bank[:, c * P : (c + 1) * P], scalar1=float(PARTICLES)
+            )
         for c in range(F_CHUNKS):
             nc.vector.tensor_scalar(
-                out=neg_send[:, c, :],
+                out=send_term[:, c, :],
                 in0=send_bank[:, c * P : (c + 1) * P],
                 scalar1=rp_bias[:, c : c + 1],
-                scalar2=-1.0,
+                scalar2=1.0 if c < POOL_CHUNKS else -1.0,
                 op0=ALU.add,
                 op1=ALU.mult,
             )
@@ -305,7 +338,7 @@ def tile_compositionalkoopmanoperators_pa_t_kernel(
         def sum_neg_send():
             nc.vector.tensor_reduce(
                 out=neg_send_sum[:],
-                in_=neg_send[:].rearrange("p c (b j) -> p (c b) j", j=PARTICLES),
+                in_=send_term[:].rearrange("p c (b j) -> p (c b) j", j=PARTICLES),
                 axis=mybir.AxisListType.X,
                 op=ALU.add,
             )
@@ -343,7 +376,15 @@ def tile_compositionalkoopmanoperators_pa_t_kernel(
             for half in range(2)
         ]
         nc.scalar.copy(out=agg[1][:], in_=agg_receiver[:].rearrange("p c n -> p n c"))
-        for c in range(F_CHUNKS):
+        joined = end_pool.tile([P, POOL_CHUNKS, 2 * P], F32, name="joined", tag="joined")
+        nc.vector.tensor_tensor(
+            out=joined[:], in0=pool_sums[:, :, 0 : 2 * P], in1=pool_sums[:, :, 2 * P : 4 * P], op=ALU.add
+        )
+        for c in range(POOL_CHUNKS):
+            nc.vector.tensor_tensor(
+                out=agg[0][:, :, c], in0=joined[:, c, 0:P], in1=joined[:, c, P : 2 * P], op=ALU.add
+            )
+        for c in range(POOL_CHUNKS, F_CHUNKS):
             for g in range(HALF_GRAPHS):
                 cols = slice(g * PARTICLES, (g + 1) * PARTICLES)
                 nc.vector.scalar_tensor_tensor(

@@ -24,7 +24,6 @@ ROUNDS = HALF_GRAPHS * PARTICLES * PARTICLES // UNIT_COLS
 F_CHUNKS = NF // P
 WORDS = NF // 2
 RUNNING = 2
-POOL_CHUNKS = 2
 X_BUFS = 5
 AHEAD = 2
 
@@ -163,39 +162,20 @@ def tile_compositionalkoopmanoperators_pa_t_kernel(
                 if c == F_CHUNKS // 2 and r + 1 < ROUNDS:
                     quantise_round(r + 1)
                 bank = mx_psum.tile([P, UNIT_COLS], F32, name="by_sender", tag="by_sender")
-                by_pool = c < POOL_CHUNKS
-                mx_pass(bank[:], columns(wr, c * P, P), columns(mx_rounds[r][0], 0, UNIT_COLS), True, by_pool)
-                if by_pool:
-                    clipped = end_pool.tile([P, UNIT_COLS], F32, name="clipped", tag="clipped", bufs=3)
-                else:
-                    mx_pass(bank[:], columns(wi, c * P, P), columns(receivers, 0, UNIT_COLS), False, True)
+                mx_pass(bank[:], columns(wr, c * P, P), columns(mx_rounds[r][0], 0, UNIT_COLS), True, False)
+                mx_pass(bank[:], columns(wi, c * P, P), columns(receivers, 0, UNIT_COLS), False, True)
                 for s in range(UNIT_BLOCKS):
                     for g in range(HALF_GRAPHS):
                         cols = slice(g * PARTICLES, (g + 1) * PARTICLES)
-                        bank_cols = slice(s * P + g * PARTICLES, s * P + (g + 1) * PARTICLES)
                         sender = g * PARTICLES + r * UNIT_BLOCKS + s
-                        if by_pool:
-                            nc.vector.scalar_tensor_tensor(
-                                out=clipped[:, bank_cols],
-                                in0=bank[:, bank_cols],
-                                scalar=send_term[:, c, sender : sender + 1],
-                                in1=neg_recv[:, c, cols],
-                                op0=ALU.add,
-                                op1=ALU.max,
-                            )
-                        else:
-                            nc.vector.scalar_tensor_tensor(
-                                out=sums[:, c, s % RUNNING, cols],
-                                in0=bank[:, bank_cols],
-                                scalar=send_term[:, c, sender : sender + 1],
-                                in1=sums[:, c, s % RUNNING, cols],
-                                op0=ALU.max,
-                                op1=ALU.add,
-                            )
-                if by_pool:
-                    nc.gpsimd.tensor_tensor(
-                        out=pool_sums[:, c, :], in0=pool_sums[:, c, :], in1=clipped[:], op=ALU.add
-                    )
+                        nc.vector.scalar_tensor_tensor(
+                            out=sums[:, c, s % RUNNING, cols],
+                            in0=bank[:, s * P + g * PARTICLES : s * P + (g + 1) * PARTICLES],
+                            scalar=neg_send[:, c, sender : sender + 1],
+                            in1=sums[:, c, s % RUNNING, cols],
+                            op0=ALU.max,
+                            op1=ALU.add,
+                        )
 
                 bank = mx_psum.tile([P, UNIT_COLS], F32, name="by_receiver", tag="by_receiver")
                 mx_pass(bank[:], columns(wr, c * P, P), columns(mx_rounds[r][1], 0, UNIT_COLS), True, False)
@@ -294,9 +274,7 @@ def tile_compositionalkoopmanoperators_pa_t_kernel(
             columns(senders, UNIT_COLS - PARTICLES, P),
         )
 
-        send_term = keep.tile([P, F_CHUNKS, P], F32, name="send_term")
-        neg_recv = keep.tile([P, POOL_CHUNKS, P], F32, name="neg_recv")
-        pool_sums = keep.tile([P, POOL_CHUNKS, UNIT_COLS], F32, name="pool_sums")
+        neg_send = keep.tile([P, F_CHUNKS, P], F32, name="neg_send")
         recv_bias = keep.tile([P, F_CHUNKS, P], F32, name="recv_bias")
         send_bank = mx_psum.tile([P, F_CHUNKS * P], F32, name="send_bank", tag="by_sender")
         recv_bank = mx_psum.tile([P, F_CHUNKS * P], F32, name="recv_bank", tag="by_receiver")
@@ -304,23 +282,12 @@ def tile_compositionalkoopmanoperators_pa_t_kernel(
             mx_pass(send_bank[:, c * P : (c + 1) * P], columns(wj, c * P, P), particles[0], True, True)
         for c in range(F_CHUNKS):
             mx_pass(recv_bank[:, c * P : (c + 1) * P], columns(wi, c * P, P), particles[1], True, True)
-        own_bank = flip_psum.tile([P, 4 * P], F32, name="own_bank", tag="flipped")
-        for c in range(POOL_CHUNKS):
-            mx_pass(own_bank[:, c * P : (c + 1) * P], columns(wi, c * P, P), particles[0], True, True)
-        nc.vector.memset(pool_sums[:, :, P:UNIT_COLS], 0.0)
-        for c in range(POOL_CHUNKS):
-            nc.vector.tensor_scalar_mul(
-                out=neg_recv[:, c, :], in0=own_bank[:, c * P : (c + 1) * P], scalar1=-1.0
-            )
-            nc.vector.tensor_scalar_mul(
-                out=pool_sums[:, c, 0:P], in0=own_bank[:, c * P : (c + 1) * P], scalar1=float(PARTICLES)
-            )
         for c in range(F_CHUNKS):
             nc.vector.tensor_scalar(
-                out=send_term[:, c, :],
+                out=neg_send[:, c, :],
                 in0=send_bank[:, c * P : (c + 1) * P],
                 scalar1=rp_bias[:, c : c + 1],
-                scalar2=1.0 if c < POOL_CHUNKS else -1.0,
+                scalar2=-1.0,
                 op0=ALU.add,
                 op1=ALU.mult,
             )
@@ -338,7 +305,7 @@ def tile_compositionalkoopmanoperators_pa_t_kernel(
         def sum_neg_send():
             nc.vector.tensor_reduce(
                 out=neg_send_sum[:],
-                in_=send_term[:].rearrange("p c (b j) -> p (c b) j", j=PARTICLES),
+                in_=neg_send[:].rearrange("p c (b j) -> p (c b) j", j=PARTICLES),
                 axis=mybir.AxisListType.X,
                 op=ALU.add,
             )
@@ -346,15 +313,16 @@ def tile_compositionalkoopmanoperators_pa_t_kernel(
         def quantise_second(name, grouped):
             second[name] = quantise_weight(name, grouped)
 
+        def pool_copy(out, in_):
+            nc.gpsimd.tensor_scalar(
+                out=out, in0=in_, scalar1=1.0, scalar2=0.0, op0=ALU.mult, op1=ALU.add
+            )
+
         chores = [sum_neg_send]
         for name, raw in (("po", po_raw), ("pa", pa_raw)):
             grouped = grouped_tile(name)
             for c in range(F_CHUNKS):
-                chores.append(
-                    lambda grouped=grouped, raw=raw, c=c: regroup_weight(
-                        grouped, raw, c * P, P, nc.scalar.copy
-                    )
-                )
+                regroup_weight(grouped, raw, c * P, P, pool_copy)
             chores.append(lambda name=name, grouped=grouped: quantise_second(name, grouped))
 
         for r in range(ROUNDS):
@@ -376,15 +344,7 @@ def tile_compositionalkoopmanoperators_pa_t_kernel(
             for half in range(2)
         ]
         nc.scalar.copy(out=agg[1][:], in_=agg_receiver[:].rearrange("p c n -> p n c"))
-        joined = end_pool.tile([P, POOL_CHUNKS, 2 * P], F32, name="joined", tag="joined")
-        nc.vector.tensor_tensor(
-            out=joined[:], in0=pool_sums[:, :, 0 : 2 * P], in1=pool_sums[:, :, 2 * P : 4 * P], op=ALU.add
-        )
-        for c in range(POOL_CHUNKS):
-            nc.vector.tensor_tensor(
-                out=agg[0][:, :, c], in0=joined[:, c, 0:P], in1=joined[:, c, P : 2 * P], op=ALU.add
-            )
-        for c in range(POOL_CHUNKS, F_CHUNKS):
+        for c in range(F_CHUNKS):
             for g in range(HALF_GRAPHS):
                 cols = slice(g * PARTICLES, (g + 1) * PARTICLES)
                 nc.vector.scalar_tensor_tensor(

@@ -25,6 +25,7 @@ F_CHUNKS = NF // P
 WORDS = NF // 2
 RUNNING = 2
 X_BUFS = 5
+SQUARE = 32
 AHEAD = 2
 
 FLOPS = 2 * NF * NF * (GRAPHS * PARTICLES * PARTICLES + 4 * GRAPHS * PARTICLES)
@@ -104,21 +105,38 @@ def tile_compositionalkoopmanoperators_pa_t_kernel(
 
         by_pair = rel_enc.rearrange("b i j k -> (b i) (j k)")
         by_relation = rel_enc.rearrange("b i j k -> (b i j) k")
+        by_half_relation = rel_enc.rearrange("b i j (u k) -> (b i j u) k", u=2)
         x_rounds = []
 
+        def on_vector(r):
+            return r % 2 == 1
+
+
         def load_round(r):
-            x_sender = x_pool.tile([P, UNIT_BLOCKS * NF], BF16, name="x_sb", tag="x_sb")
+            x_sender = x_pool.tile([P, UNIT_BLOCKS * NF], BF16, name="x_sb", tag="x_sb", align_bytes=64)
             first = r * UNIT_BLOCKS * NF
             nc.sync.dma_start(out=x_sender[:], in_=by_pair[0:P, first : first + UNIT_BLOCKS * NF])
-            x_receiver = x_pool.tile([P, UNIT_BLOCKS * NF], BF16, name="x_sb", tag="x_sb")
             first = (ROUNDS + r) * UNIT_COLS
-            nc.sync.dma_start(
-                out=x_receiver[:].rearrange("p (s k) -> p s k", s=UNIT_BLOCKS),
-                in_=by_relation[first : first + UNIT_COLS, :].rearrange("(s p) k -> p s k", p=P),
-            )
+            if on_vector(r):
+                x_receiver = x_pool.tile([P, UNIT_BLOCKS * NF], BF16, name="x_sb", tag="x_sb", align_bytes=64)
+                for a in range(P // SQUARE):
+                    nc.sync.dma_start(
+                        out=x_receiver[a * SQUARE : (a + 1) * SQUARE, :].rearrange(
+                            "p (s k) -> p s k", k=2 * SQUARE
+                        ),
+                        in_=by_half_relation[
+                            2 * first : 2 * (first + UNIT_COLS), 2 * a * SQUARE : 2 * (a + 1) * SQUARE
+                        ].rearrange("(s p) k -> p s k", p=SQUARE),
+                    )
+            else:
+                x_receiver = x_pool.tile([P, UNIT_BLOCKS * NF], BF16, name="x_sb", tag="x_sb", align_bytes=64)
+                nc.sync.dma_start(
+                    out=x_receiver[:].rearrange("p (s k) -> p s k", s=UNIT_BLOCKS),
+                    in_=by_relation[first : first + UNIT_COLS, :].rearrange("(s p) k -> p s k", p=P),
+                )
             x_rounds.append((x_sender, x_receiver))
 
-        def transpose_unit(x_sb, copy):
+        def transpose_unit(x_sb, *copies):
             x_words = x_sb[:].bitcast(F32)
             grouped = q_pool.tile(
                 [P, UNIT_COLS * PACK], BF16, name="grouped", tag="grouped", align_bytes=64
@@ -130,7 +148,7 @@ def tile_compositionalkoopmanoperators_pa_t_kernel(
                     for u in range(2):
                         first = (2 * pair + s) * WORDS + u * P
                         transpose_words(bank, 2 * s + u, x_words[:, first : first + P])
-                copy(
+                copies[pair](
                     out=grouped_words[:, pair * 4 * P : (pair + 1) * 4 * P].rearrange(
                         "q (s c u) -> q s c u", s=2, u=2
                     ),
@@ -138,15 +156,31 @@ def tile_compositionalkoopmanoperators_pa_t_kernel(
                 )
             return grouped
 
+        def transpose_unit_on_vector(x_sb):
+            grouped = q_pool.tile(
+                [P, UNIT_COLS * PACK], BF16, name="grouped", tag="grouped", align_bytes=64
+            )
+            nc.vector.transpose(grouped[:].bitcast(F32), x_sb[:].bitcast(F32))
+            return grouped
+
         grouped_rounds = []
 
         def transpose_round(r):
-            grouped_rounds.append(
-                (
-                    transpose_unit(x_rounds[r][0], nc.vector.tensor_copy),
-                    transpose_unit(x_rounds[r][1], nc.scalar.copy),
+            x_sender, x_receiver = x_rounds[r]
+            if on_vector(r):
+                grouped_rounds.append(
+                    (
+                        transpose_unit(x_sender, nc.scalar.copy, nc.scalar.copy),
+                        transpose_unit_on_vector(x_receiver),
+                    )
                 )
-            )
+            else:
+                grouped_rounds.append(
+                    (
+                        transpose_unit(x_sender, nc.vector.tensor_copy, nc.scalar.copy),
+                        transpose_unit(x_receiver, nc.scalar.copy, nc.scalar.copy),
+                    )
+                )
 
         mx_rounds = []
 

@@ -5,6 +5,7 @@ from concourse.masks import make_identity
 
 F32 = mybir.dt.float32
 BF16 = mybir.dt.bfloat16
+I32 = mybir.dt.int32
 U32 = mybir.dt.uint32
 U8 = mybir.dt.uint8
 FP8X4 = mybir.dt.float8_e4m3fn_x4
@@ -24,7 +25,8 @@ ROUNDS = HALF_GRAPHS * PARTICLES * PARTICLES // UNIT_COLS
 F_CHUNKS = NF // P
 WORDS = NF // 2
 RUNNING = 2
-X_BUFS = 5
+X_BUFS = 7
+ON_VECTOR_FROM = 4
 SQUARE = 32
 AHEAD = 2
 
@@ -39,7 +41,8 @@ def tile_compositionalkoopmanoperators_pa_t_kernel(
         stack.enter_context(tc.manual_schedule())
         keep = stack.enter_context(tc.tile_pool(name="keep", bufs=1))
         x_pool = stack.enter_context(tc.tile_pool(name="x_pool", bufs=2 * X_BUFS))
-        q_pool = stack.enter_context(tc.tile_pool(name="q_pool", bufs=2 * AHEAD))
+        grouped_pool = stack.enter_context(tc.tile_pool(name="grouped_pool", bufs=7))
+        q_pool = stack.enter_context(tc.tile_pool(name="q_pool", bufs=4))
         end_pool = stack.enter_context(tc.tile_pool(name="end_pool", bufs=2))
         flip_psum = stack.enter_context(tc.psum_pool(name="flip_psum", bufs=4))
         mx_psum = stack.enter_context(tc.psum_pool(name="mx_psum", bufs=2))
@@ -89,11 +92,6 @@ def tile_compositionalkoopmanoperators_pa_t_kernel(
                 .rearrange("p t (c i) -> p c t i", i=4),
             )
 
-        def quantise_weight(name, grouped):
-            mx = mx_tiles(keep, name, NF)
-            quantise(columns(mx, 0, NF), grouped[:])
-            return mx
-
         def word_order(w):
             return w.rearrange("(u q e) n -> q u (e n)", u=2, e=2)
 
@@ -109,19 +107,25 @@ def tile_compositionalkoopmanoperators_pa_t_kernel(
         x_rounds = []
 
         def on_vector(r):
-            return r % 2 == 1
+            return r >= ON_VECTOR_FROM
 
 
-        def load_round(r):
-            x_sender = x_pool.tile([P, UNIT_BLOCKS * NF], BF16, name="x_sb", tag="x_sb", align_bytes=64)
+        def x_tile():
+            return x_pool.tile([P, UNIT_BLOCKS * NF], BF16, name="x_sb", tag="x_sb", align_bytes=64)
+
+        def load_sender_unit(r):
+            x_sb = x_tile()
             first = r * UNIT_BLOCKS * NF
-            nc.sync.dma_start(out=x_sender[:], in_=by_pair[0:P, first : first + UNIT_BLOCKS * NF])
+            nc.sync.dma_start(out=x_sb[:], in_=by_pair[0:P, first : first + UNIT_BLOCKS * NF])
+            return x_sb
+
+        def load_receiver_unit(r):
+            x_sb = x_tile()
             first = (ROUNDS + r) * UNIT_COLS
             if on_vector(r):
-                x_receiver = x_pool.tile([P, UNIT_BLOCKS * NF], BF16, name="x_sb", tag="x_sb", align_bytes=64)
                 for a in range(P // SQUARE):
                     nc.sync.dma_start(
-                        out=x_receiver[a * SQUARE : (a + 1) * SQUARE, :].rearrange(
+                        out=x_sb[a * SQUARE : (a + 1) * SQUARE, :].rearrange(
                             "p (s k) -> p s k", k=2 * SQUARE
                         ),
                         in_=by_half_relation[
@@ -129,16 +133,18 @@ def tile_compositionalkoopmanoperators_pa_t_kernel(
                         ].rearrange("(s p) k -> p s k", p=SQUARE),
                     )
             else:
-                x_receiver = x_pool.tile([P, UNIT_BLOCKS * NF], BF16, name="x_sb", tag="x_sb", align_bytes=64)
                 nc.sync.dma_start(
-                    out=x_receiver[:].rearrange("p (s k) -> p s k", s=UNIT_BLOCKS),
+                    out=x_sb[:].rearrange("p (s k) -> p s k", s=UNIT_BLOCKS),
                     in_=by_relation[first : first + UNIT_COLS, :].rearrange("(s p) k -> p s k", p=P),
                 )
-            x_rounds.append((x_sender, x_receiver))
+            return x_sb
+
+        def load_round(r):
+            x_rounds.append([load_sender_unit(r), load_receiver_unit(r)])
 
         def transpose_unit(x_sb, *copies):
             x_words = x_sb[:].bitcast(F32)
-            grouped = q_pool.tile(
+            grouped = grouped_pool.tile(
                 [P, UNIT_COLS * PACK], BF16, name="grouped", tag="grouped", align_bytes=64
             )
             grouped_words = grouped[:].bitcast(F32)
@@ -157,244 +163,304 @@ def tile_compositionalkoopmanoperators_pa_t_kernel(
             return grouped
 
         def transpose_unit_on_vector(x_sb):
-            grouped = q_pool.tile(
+            grouped = grouped_pool.tile(
                 [P, UNIT_COLS * PACK], BF16, name="grouped", tag="grouped", align_bytes=64
             )
             nc.vector.transpose(grouped[:].bitcast(F32), x_sb[:].bitcast(F32))
             return grouped
 
-        grouped_rounds = []
+        grouped_units = {}
 
-        def transpose_round(r):
-            x_sender, x_receiver = x_rounds[r]
+        def transpose_sender(r):
+            first_copy = nc.scalar.copy if on_vector(r) else nc.vector.tensor_copy
+            grouped_units[r, 0] = transpose_unit(x_rounds[r][0], first_copy, nc.scalar.copy)
+
+        def transpose_receiver(r):
             if on_vector(r):
-                grouped_rounds.append(
-                    (
-                        transpose_unit(x_sender, nc.scalar.copy, nc.scalar.copy),
-                        transpose_unit_on_vector(x_receiver),
-                    )
-                )
+                grouped_units[r, 1] = transpose_unit_on_vector(x_rounds[r][1])
             else:
-                grouped_rounds.append(
-                    (
-                        transpose_unit(x_sender, nc.vector.tensor_copy, nc.scalar.copy),
-                        transpose_unit(x_receiver, nc.scalar.copy, nc.scalar.copy),
-                    )
-                )
+                grouped_units[r, 1] = transpose_unit(x_rounds[r][1], nc.scalar.copy, nc.scalar.copy)
+
+        def transpose_ahead(r):
+            r += AHEAD
+            if r >= ROUNDS:
+                return
+            if not on_vector(r):
+                transpose_sender(r)
+            elif (r - ON_VECTOR_FROM) % 2 == 0:
+                transpose_sender(r)
+                transpose_sender(r + 1)
+            transpose_receiver(r)
 
         mx_rounds = []
 
+        def quantise_unit(grouped):
+            mx = mx_tiles(q_pool, "x", UNIT_COLS)
+            quantise(columns(mx, 0, UNIT_COLS), grouped[:])
+            return mx
+
         def quantise_round(r):
-            pair = [mx_tiles(q_pool, "x", UNIT_COLS) for kind in range(2)]
-            for kind in (1, 0):
-                quantise(columns(pair[kind], 0, UNIT_COLS), grouped_rounds[r][kind][:])
-            mx_rounds.append(pair)
+            mx_rounds.append([quantise_unit(grouped_units[r, kind]) for kind in range(2)])
+
+        def sender_products(r, c):
+            bank = mx_psum.tile([P, UNIT_COLS], F32, name="by_sender", tag="by_sender")
+            moving = columns(mx_rounds[r][0], 0, UNIT_COLS)
+            mx_pass(bank[:], columns(wr, c * P, P), moving, True, False)
+            mx_pass(bank[:], columns(wi, c * P, P), columns(receivers, 0, UNIT_COLS), False, True)
+            return bank
+
+        def receiver_products(r, c):
+            bank = mx_psum.tile([P, UNIT_COLS], F32, name="by_receiver", tag="by_receiver")
+            graph = r * UNIT_SLICES // PARTICLES
+            moving = columns(mx_rounds[r][1], 0, UNIT_COLS)
+            mx_pass(bank[:], columns(wr, c * P, P), moving, True, False)
+            mx_pass(bank[:], columns(wj, c * P, P), columns(senders[graph], 0, UNIT_COLS), False, True)
+            return bank
+
+        def add_by_sender(r, c, bank):
+            for s in range(UNIT_BLOCKS):
+                for g in range(HALF_GRAPHS):
+                    cols = slice(g * PARTICLES, (g + 1) * PARTICLES)
+                    sender = g * PARTICLES + r * UNIT_BLOCKS + s
+                    nc.vector.scalar_tensor_tensor(
+                        out=sums[:, s % RUNNING, c, cols],
+                        in0=bank[:, s * P + g * PARTICLES : s * P + (g + 1) * PARTICLES],
+                        scalar=neg_send[:, c, sender : sender + 1],
+                        in1=sums[:, s % RUNNING, c, cols],
+                        op0=ALU.max,
+                        op1=ALU.add,
+                    )
+
+        def add_by_receiver(r, c, bank):
+            effects = end_pool.tile([P, UNIT_COLS], F32, name="effects", tag="effects")
+            for i in range(UNIT_SLICES):
+                cols = slice(i * PARTICLES, (i + 1) * PARTICLES)
+                receiver = r * UNIT_SLICES + i
+                nc.scalar.activation(
+                    out=effects[:, cols],
+                    in_=bank[:, cols],
+                    func=ACT.Relu,
+                    bias=recv_bias[:, c, receiver : receiver + 1],
+                    accum_out=agg_receiver[:, c, receiver : receiver + 1],
+                )
 
         def multiply_round(r):
-            graph = r * UNIT_SLICES // PARTICLES
             for c in range(F_CHUNKS):
+                sender_bank = sender_products(r, c)
+                receiver_bank = receiver_products(r, c)
                 if c == F_CHUNKS // 2 and r + 1 < ROUNDS:
                     quantise_round(r + 1)
-                bank = mx_psum.tile([P, UNIT_COLS], F32, name="by_sender", tag="by_sender")
-                mx_pass(bank[:], columns(wr, c * P, P), columns(mx_rounds[r][0], 0, UNIT_COLS), True, False)
-                mx_pass(bank[:], columns(wi, c * P, P), columns(receivers, 0, UNIT_COLS), False, True)
-                for s in range(UNIT_BLOCKS):
-                    for g in range(HALF_GRAPHS):
-                        cols = slice(g * PARTICLES, (g + 1) * PARTICLES)
-                        sender = g * PARTICLES + r * UNIT_BLOCKS + s
-                        nc.vector.scalar_tensor_tensor(
-                            out=sums[:, c, s % RUNNING, cols],
-                            in0=bank[:, s * P + g * PARTICLES : s * P + (g + 1) * PARTICLES],
-                            scalar=neg_send[:, c, sender : sender + 1],
-                            in1=sums[:, c, s % RUNNING, cols],
-                            op0=ALU.max,
-                            op1=ALU.add,
-                        )
-
-                bank = mx_psum.tile([P, UNIT_COLS], F32, name="by_receiver", tag="by_receiver")
-                mx_pass(bank[:], columns(wr, c * P, P), columns(mx_rounds[r][1], 0, UNIT_COLS), True, False)
-                mx_pass(
-                    bank[:], columns(wj, c * P, P), columns(senders, graph * UNIT_COLS, UNIT_COLS), False, True
-                )
-                effects = end_pool.tile([P, UNIT_COLS], F32, name="effects", tag="effects")
-                for i in range(UNIT_SLICES):
-                    cols = slice(i * PARTICLES, (i + 1) * PARTICLES)
-                    receiver = r * UNIT_SLICES + i
-                    nc.scalar.activation(
-                        out=effects[:, cols],
-                        in_=bank[:, cols],
-                        func=ACT.Relu,
-                        bias=recv_bias[:, c, receiver : receiver + 1],
-                        accum_out=agg_receiver[:, c, receiver : receiver + 1],
-                    )
+                add_by_sender(r, c, sender_bank)
+                add_by_receiver(r, c, receiver_bank)
 
         out_rows = out.rearrange("b i n -> (b i) n")
 
         bias_rows = keep.tile([P, P], BF16, name="bias_rows")
         nc.vector.memset(bias_rows[:], 0.0)
-        sums = keep.tile([P, F_CHUNKS, RUNNING, P], F32, name="sums")
-        nc.vector.memset(sums[:], 0.0)
         ident = keep.tile([P, P], F32, name="ident")
         make_identity(nc, ident[:])
+        sums = keep.tile([P, RUNNING, F_CHUNKS, P], F32, name="sums")
+        nc.gpsimd.memset(sums[:, 0], 0.0)
 
         obj_sb = keep.tile([P, 2 * NF], BF16, name="obj_sb")
+        nc.scalar.dma_start(out=bias_rows[0:F_CHUNKS, :], in_=rp_b.rearrange("(c p) -> c p", p=P))
+        x_rounds.append([load_sender_unit(0)])
         nc.sync.dma_start(
             out=obj_sb[:].rearrange("p (h k) -> p h k", h=2),
             in_=obj.rearrange("b i k -> (b i) k").rearrange("(h p) k -> p h k", p=P),
         )
-        nc.scalar.dma_start(out=bias_rows[0:F_CHUNKS, :], in_=rp_b.rearrange("(c p) -> c p", p=P))
-        wi_raw = load_weight("wi", word_order(rp_w[NF : 2 * NF, :]))
         wr_raw = load_weight("wr", word_order(rp_w[0:NF, :]))
+        x_rounds[0].append(load_receiver_unit(0))
         wj_raw = load_weight("wj", word_order(rp_w[2 * NF : 3 * NF, :]))
-        for r in range(X_BUFS):
+        wi_raw = load_weight("wi", word_order(rp_w[NF : 2 * NF, :]))
+        for r in range(1, X_BUFS):
             load_round(r)
         po_raw = load_weight("po", word_order(pp_w[0:NF, :]))
         pa_raw = load_weight("pa", chunk_order(pp_w[NF : 2 * NF, :]))
         pp_bias = keep.tile([P, NF], BF16, name="pp_bias")
         nc.sync.dma_start(out=pp_bias[:], in_=pp_b.partition_broadcast(P))
 
+        transpose_sender(0)
+
         obj_words = obj_sb[:].bitcast(F32)
-        obj_banks = []
-        for half, tag in enumerate(("by_sender", "by_receiver")):
-            obj_bank = mx_psum.tile([P, 4 * P], F32, name="obj_bank", tag=tag)
+        obj_bank = mx_psum.tile([P, 4 * P], F32, name="obj_bank", tag="by_sender")
+        for half in range(2):
             for u in range(2):
                 first = half * WORDS + u * P
-                transpose_words(obj_bank, u, obj_words[:, first : first + P])
-            obj_banks.append(obj_bank)
-
-        def repeat(name, first, count):
-            half, col = divmod(first, P)
-            times = UNIT_COLS // count
-            rep = keep.tile([P, UNIT_COLS * PACK], BF16, name=name, align_bytes=64)
-            nc.scalar.copy(
-                out=rep[:].bitcast(F32).rearrange("q (r c u) -> q r c u", r=times, u=2),
-                in_=obj_banks[half][:, 0 : 2 * P]
-                .rearrange("q (u c) -> q c u", u=2)[:, col : col + count, :]
-                .unsqueeze(1)
-                .to_broadcast([P, times, count, 2]),
-            )
-            return rep
-
-        receivers_rep = repeat("receivers_rep", 0, P)
-        senders_rep = [
-            repeat("senders_rep%d" % g, P + g * PARTICLES, PARTICLES) for g in range(HALF_GRAPHS)
-        ]
-        receivers = mx_tiles(keep, "receivers", UNIT_COLS)
-        senders = mx_tiles(keep, "senders", HALF_GRAPHS * UNIT_COLS)
+                transpose_words(obj_bank, 2 * half + u, obj_words[:, first : first + P])
+        particles_grouped = keep.tile(
+            [P, GRAPHS * PARTICLES * PACK], BF16, name="particles_grouped", align_bytes=64
+        )
+        particle_words = particles_grouped[:].bitcast(F32)
+        nc.scalar.copy(
+            out=particle_words.rearrange("q (h c u) -> q h c u", h=2, u=2),
+            in_=obj_bank[:].rearrange("q (h u c) -> q h c u", h=2, u=2),
+        )
 
         bias_f32 = keep.tile([P, P], F32, name="bias_f32")
         nc.vector.tensor_copy(out=bias_f32[:], in_=bias_rows[:])
-        bias_bank = mx_psum.tile([P, 4 * P], F32, name="bias_bank", tag="by_sender")
+        bias_bank = mx_psum.tile([P, 4 * P], F32, name="bias_bank", tag="by_receiver")
         transpose_words(bias_bank, 0, bias_f32[:])
         rp_bias = keep.tile([P, F_CHUNKS], F32, name="rp_bias")
+        neg_rp_bias = keep.tile([P, F_CHUNKS], F32, name="neg_rp_bias")
+        nc.scalar.copy(out=rp_bias[:], in_=bias_bank[:, 0:F_CHUNKS])
+        nc.scalar.mul(neg_rp_bias[:], rp_bias[:], -1.0)
 
-        wi_grouped, wr_grouped, wj_grouped = grouped_tile("wi"), grouped_tile("wr"), grouped_tile("wj")
-        regroup_weight(wi_grouped, wi_raw, 0, NF, nc.vector.tensor_copy)
-        quantise(columns(receivers, 0, UNIT_COLS), receivers_rep[:])
-        regroup_weight(wr_grouped, wr_raw, 0, NF, nc.vector.tensor_copy)
-        regroup_weight(wj_grouped, wj_raw, 0, NF, nc.scalar.copy)
-        nc.vector.tensor_copy(out=rp_bias[:], in_=bias_bank[:, 0:F_CHUNKS])
-        for g in range(HALF_GRAPHS):
-            quantise(columns(senders, g * UNIT_COLS, UNIT_COLS), senders_rep[g][:])
-        wi = quantise_weight("wi", wi_grouped)
-        wr = quantise_weight("wr", wr_grouped)
-        transpose_round(0)
-        wj = quantise_weight("wj", wj_grouped)
-        quantise_round(0)
-        transpose_round(1)
+        def repeated(name, first, count):
+            times = UNIT_COLS // count
+            mx = mx_tiles(keep, name, UNIT_COLS)
+            for to, source in zip(mx, columns(particles, first, count)):
+                words = source.bitcast(I32)
+                nc.vector.tensor_copy(
+                    out=to[:].bitcast(I32).rearrange("q (r w) -> q r w", r=times),
+                    in_=words.unsqueeze(1).to_broadcast([P, times, words.shape[1]]),
+                )
+            return mx
 
-        particles = (
-            columns(receivers, 0, P),
-            columns(senders, UNIT_COLS - PARTICLES, P),
-        )
+        weights = {}
+
+        def weight_tiles(name, raw):
+            weights[name] = (raw, grouped_tile(name), mx_tiles(keep, name, NF))
+            return weights[name][2]
+
+        def regroup_chunk(name, c, copy):
+            raw, grouped, mx = weights[name]
+            regroup_weight(grouped, raw, c * P, P, copy)
+
+        def quantise_chunk(name, c):
+            raw, grouped, mx = weights[name]
+            quantise(columns(mx, c * P, P), grouped[:, c * P * PACK : (c + 1) * P * PACK])
+
+        wr = weight_tiles("wr", wr_raw)
+        wj = weight_tiles("wj", wj_raw)
+        wi = weight_tiles("wi", wi_raw)
+        particles = mx_tiles(keep, "particles", GRAPHS * PARTICLES)
+
+        transpose_receiver(0)
+        mx_rounds.append([quantise_unit(grouped_units[0, 0])])
+        quantise(columns(particles, 0, GRAPHS * PARTICLES), particles_grouped[:])
+        for c in range(F_CHUNKS):
+            regroup_chunk("wr", c, nc.vector.tensor_copy)
+        for c in range(F_CHUNKS):
+            regroup_chunk("wj", c, nc.scalar.copy)
+        receivers = repeated("receivers", 0, P)
+        senders = [
+            repeated("senders%d" % g, P + g * PARTICLES, PARTICLES) for g in range(HALF_GRAPHS)
+        ]
+        mx_rounds[0].append(quantise_unit(grouped_units[0, 1]))
+        quantise_chunk("wr", 0)
+        regroup_chunk("wi", 0, nc.vector.tensor_copy)
+        for name in ("wj", "wi"):
+            quantise_chunk(name, 0)
 
         neg_send = keep.tile([P, F_CHUNKS, P], F32, name="neg_send")
         recv_bias = keep.tile([P, F_CHUNKS, P], F32, name="recv_bias")
-        send_bank = mx_psum.tile([P, F_CHUNKS * P], F32, name="send_bank", tag="by_sender")
-        recv_bank = mx_psum.tile([P, F_CHUNKS * P], F32, name="recv_bank", tag="by_receiver")
-        for c in range(F_CHUNKS):
-            mx_pass(send_bank[:, c * P : (c + 1) * P], columns(wj, c * P, P), particles[0], True, True)
-        for c in range(F_CHUNKS):
-            mx_pass(recv_bank[:, c * P : (c + 1) * P], columns(wi, c * P, P), particles[1], True, True)
-        for c in range(F_CHUNKS):
-            nc.vector.tensor_scalar(
-                out=neg_send[:, c, :],
-                in0=send_bank[:, c * P : (c + 1) * P],
-                scalar1=rp_bias[:, c : c + 1],
-                scalar2=-1.0,
-                op0=ALU.add,
-                op1=ALU.mult,
+        neg_send_sum = keep.tile([P, F_CHUNKS, HALF_GRAPHS], F32, name="neg_send_sum")
+        agg_receiver = keep.tile([P, F_CHUNKS, P], F32, name="agg_receiver")
+
+        def particle_products(c):
+            send_bank = flip_psum.tile([P, 4 * P], F32, name="send_bank", tag="flipped")
+            mx_pass(send_bank[:, 0:P], columns(wj, c * P, P), columns(particles, 0, P), True, True)
+            recv_bank = flip_psum.tile([P, 4 * P], F32, name="recv_bank", tag="flipped")
+            mx_pass(recv_bank[:, 0:P], columns(wi, c * P, P), columns(particles, P, P), True, True)
+            for g in range(HALF_GRAPHS):
+                cols = slice(g * PARTICLES, (g + 1) * PARTICLES)
+                nc.scalar.activation(
+                    out=neg_send[:, c, cols],
+                    in_=send_bank[:, cols],
+                    func=ACT.Identity,
+                    scale=-1.0,
+                    bias=neg_rp_bias[:, c : c + 1],
+                    accum_out=neg_send_sum[:, c, g : g + 1],
+                )
+            nc.scalar.activation(
+                out=sums[:, 1, c, :].rearrange("p (b n) -> p b n", b=HALF_GRAPHS),
+                in_=neg_send_sum[:, c, :].unsqueeze(2).to_broadcast([P, HALF_GRAPHS, PARTICLES]),
+                func=ACT.Copy,
+                scale=-1.0,
             )
             nc.scalar.activation(
                 out=recv_bias[:, c, :],
-                in_=recv_bank[:, c * P : (c + 1) * P],
+                in_=recv_bank[:, 0:P],
                 func=ACT.Identity,
                 bias=rp_bias[:, c : c + 1],
             )
-        agg_receiver = keep.tile([P, F_CHUNKS, P], F32, name="agg_receiver")
 
-        neg_send_sum = keep.tile([P, F_CHUNKS * HALF_GRAPHS], F32, name="neg_send_sum")
-        second = {}
+        def prepare_chunk(c):
+            regroup_chunk("wi", c, nc.vector.tensor_copy)
+            for name in ("wr", "wj", "wi"):
+                quantise_chunk(name, c)
 
-        def sum_neg_send():
-            nc.vector.tensor_reduce(
-                out=neg_send_sum[:],
-                in_=neg_send[:].rearrange("p c (b j) -> p (c b) j", j=PARTICLES),
-                axis=mybir.AxisListType.X,
-                op=ALU.add,
-            )
+        particle_products(0)
+        prepare_chunk(1)
 
-        def quantise_second(name, grouped):
-            second[name] = quantise_weight(name, grouped)
-
-        def pool_copy(out, in_):
-            nc.gpsimd.tensor_scalar(
-                out=out, in0=in_, scalar1=1.0, scalar2=0.0, op0=ALU.mult, op1=ALU.add
-            )
-
-        chores = [sum_neg_send]
-        for name, raw in (("po", po_raw), ("pa", pa_raw)):
-            grouped = grouped_tile(name)
+        po = weight_tiles("po", po_raw)
+        pa = weight_tiles("pa", pa_raw)
+        chores = []
+        for name in ("po", "pa"):
             for c in range(F_CHUNKS):
-                regroup_weight(grouped, raw, c * P, P, pool_copy)
-            chores.append(lambda name=name, grouped=grouped: quantise_second(name, grouped))
+                chores.append(lambda name=name, c=c: regroup_chunk(name, c, nc.scalar.copy))
+        for name in ("po", "pa"):
+            chores.append(lambda name=name: quantise_whole(name))
+
+        def quantise_whole(name):
+            raw, grouped, mx = weights[name]
+            quantise(columns(mx, 0, NF), grouped[:])
+
+        def first_round():
+            for c in range(F_CHUNKS):
+                sender_bank = sender_products(0, c)
+                receiver_bank = receiver_products(0, c)
+                if c + 1 < F_CHUNKS:
+                    particle_products(c + 1)
+                add_by_sender(0, c, sender_bank)
+                if c + 2 < F_CHUNKS:
+                    prepare_chunk(c + 2)
+                add_by_receiver(0, c, receiver_bank)
+                if c == 1:
+                    transpose_sender(1)
+                    transpose_receiver(1)
+                if c == 2:
+                    quantise_round(1)
 
         for r in range(ROUNDS):
-            multiply_round(r)
-            if r + AHEAD < ROUNDS:
-                transpose_round(r + AHEAD)
+            if r == 0:
+                first_round()
+            else:
+                multiply_round(r)
+            transpose_ahead(r)
             if r + X_BUFS < ROUNDS:
                 load_round(r + X_BUFS)
-            if r < len(chores):
-                chores[r]()
+            if r >= ROUNDS - len(chores) - 1 and chores:
+                chores.pop(0)()
 
         banks = []
         for half in range(2):
             bank = flip_psum.tile([P, NF], F32, name="particle", tag="flipped")
-            mx_pass(bank[:], particles[half], columns(second["po"], 0, NF), True, False)
+            mx_pass(bank[:], columns(particles, half * P, P), columns(po, 0, NF), True, False)
             banks.append(bank)
         agg = [
             end_pool.tile([P, P, PACK], BF16, name="agg%d" % half, tag="agg%d" % half, align_bytes=64)
             for half in range(2)
         ]
         nc.scalar.copy(out=agg[1][:], in_=agg_receiver[:].rearrange("p c n -> p n c"))
-        for c in range(F_CHUNKS):
-            for g in range(HALF_GRAPHS):
-                cols = slice(g * PARTICLES, (g + 1) * PARTICLES)
-                nc.vector.scalar_tensor_tensor(
-                    out=agg[0][:, cols, c],
-                    in0=sums[:, c, 0, cols],
-                    scalar=neg_send_sum[:, c * HALF_GRAPHS + g : c * HALF_GRAPHS + g + 1],
-                    in1=sums[:, c, 1, cols],
-                    op0=ALU.subtract,
-                    op1=ALU.add,
-                )
+        nc.vector.tensor_tensor(
+            out=agg[0][:],
+            in0=sums[:, 0].rearrange("p c n -> p n c"),
+            in1=sums[:, 1].rearrange("p c n -> p n c"),
+            op=ALU.add,
+        )
         agg_mx = [mx_tiles(keep, "agg%d" % half, P) for half in range(2)]
         for half in (1, 0):
             quantise(columns(agg_mx[half], 0, P), agg[half][:].rearrange("p c t -> p (c t)"))
+        half_cols = NF // 2
         for half in (1, 0):
-            mx_pass(banks[half][:], columns(agg_mx[half], 0, P), columns(second["pa"], 0, NF), False, True)
-            result = end_pool.tile([P, NF], F32, name="result", tag="result")
-            nc.vector.tensor_tensor(out=result[:], in0=banks[half][:], in1=pp_bias[:], op=ALU.add)
-            nc.scalar.activation(out=result[:], in_=result[:], func=ACT.Relu)
-            nc.sync.dma_start(out=out_rows[half * P : (half + 1) * P, :], in_=result[:])
+            mx_pass(banks[half][:], columns(agg_mx[half], 0, P), columns(pa, 0, NF), False, True)
+            for part in range(2):
+                cols = slice(part * half_cols, (part + 1) * half_cols)
+                result = keep.tile([P, half_cols], F32, name="result%d%d" % (half, part))
+                nc.vector.tensor_tensor(
+                    out=result[:], in0=banks[half][:, cols], in1=pp_bias[:, cols], op=ALU.add
+                )
+                nc.scalar.activation(out=result[:], in_=result[:], func=ACT.Relu)
+                nc.sync.dma_start(out=out_rows[half * P : (half + 1) * P, cols], in_=result[:])

@@ -26,8 +26,8 @@ F_CHUNKS = NF // P
 WORDS = NF // 2
 RUNNING = 2
 X_BUFS = 7
-ON_VECTOR_FROM = 4
 SQUARE = 32
+QPOS = ((2, 0), (1, 0))
 AHEAD = 2
 
 FLOPS = 2 * NF * NF * (GRAPHS * PARTICLES * PARTICLES + 4 * GRAPHS * PARTICLES)
@@ -48,9 +48,11 @@ def tile_compositionalkoopmanoperators_pa_t_kernel(
         mx_psum = stack.enter_context(tc.psum_pool(name="mx_psum", bufs=2))
 
         def mx_tiles(pool, name, cols):
-            codes = pool.tile([P, cols], U32, name=name + "_codes", tag=name + "_codes", align_bytes=64)
+            codes = pool.tile(
+                [P, cols], U32, name=name + "_codes", tag=name + "_codes", align_bytes=256
+            )
             scales = pool.tile(
-                [P, cols], U8, name=name + "_scales", tag=name + "_scales", align_bytes=64
+                [P, cols], U8, name=name + "_scales", tag=name + "_scales", align_bytes=256
             )
             return codes, scales
 
@@ -107,7 +109,7 @@ def tile_compositionalkoopmanoperators_pa_t_kernel(
         x_rounds = []
 
         def on_vector(r):
-            return r >= ON_VECTOR_FROM
+            return r % 2 == 1
 
 
         def x_tile():
@@ -154,13 +156,21 @@ def tile_compositionalkoopmanoperators_pa_t_kernel(
                     for u in range(2):
                         first = (2 * pair + s) * WORDS + u * P
                         transpose_words(bank, 2 * s + u, x_words[:, first : first + P])
-                copies[pair](
-                    out=grouped_words[:, pair * 4 * P : (pair + 1) * 4 * P].rearrange(
-                        "q (s c u) -> q s c u", s=2, u=2
-                    ),
-                    in_=bank[:].rearrange("q (s u c) -> q s c u", s=2, u=2),
+                waiting_copies.append(
+                    lambda copy=copies[pair], pair=pair, bank=bank: copy(
+                        out=grouped_words[:, pair * 4 * P : (pair + 1) * 4 * P].rearrange(
+                            "q (s c u) -> q s c u", s=2, u=2
+                        ),
+                        in_=bank[:].rearrange("q (s u c) -> q s c u", s=2, u=2),
+                    )
                 )
             return grouped
+
+        waiting_copies = []
+
+        def copy_waiting(count):
+            for i in range(min(count, len(waiting_copies))):
+                waiting_copies.pop(0)()
 
         def transpose_unit_on_vector(x_sb):
             grouped = grouped_pool.tile(
@@ -185,12 +195,10 @@ def tile_compositionalkoopmanoperators_pa_t_kernel(
             r += AHEAD
             if r >= ROUNDS:
                 return
-            if not on_vector(r):
-                transpose_sender(r)
-            elif (r - ON_VECTOR_FROM) % 2 == 0:
-                transpose_sender(r)
-                transpose_sender(r + 1)
+            transpose_sender(r)
             transpose_receiver(r)
+            if not on_vector(r):
+                copy_waiting(4)
 
         mx_rounds = []
 
@@ -198,6 +206,13 @@ def tile_compositionalkoopmanoperators_pa_t_kernel(
             mx = mx_tiles(q_pool, "x", UNIT_COLS)
             quantise(columns(mx, 0, UNIT_COLS), grouped[:])
             return mx
+
+        def quantise_at(r, c, pos):
+            if c == 0 and pos == 0:
+                mx_rounds.append([None, None])
+            for kind in (1, 0):
+                if QPOS[kind] == (c, pos):
+                    mx_rounds[r][kind] = quantise_unit(grouped_units[r, kind])
 
         def quantise_round(r):
             mx_rounds.append([quantise_unit(grouped_units[r, kind]) for kind in range(2)])
@@ -248,9 +263,12 @@ def tile_compositionalkoopmanoperators_pa_t_kernel(
             for c in range(F_CHUNKS):
                 sender_bank = sender_products(r, c)
                 receiver_bank = receiver_products(r, c)
-                if c == F_CHUNKS // 2 and r + 1 < ROUNDS:
-                    quantise_round(r + 1)
+                copy_waiting((2, 1, 1, 0)[c])
+                if r + 1 < ROUNDS:
+                    quantise_at(r + 1, c, 0)
                 add_by_sender(r, c, sender_bank)
+                if r + 1 < ROUNDS:
+                    quantise_at(r + 1, c, 1)
                 add_by_receiver(r, c, receiver_bank)
 
         out_rows = out.rearrange("b i n -> (b i) n")
@@ -281,6 +299,8 @@ def tile_compositionalkoopmanoperators_pa_t_kernel(
         nc.sync.dma_start(out=pp_bias[:], in_=pp_b.partition_broadcast(P))
 
         transpose_sender(0)
+
+        copy_waiting(2)
 
         obj_words = obj_sb[:].bitcast(F32)
         obj_bank = mx_psum.tile([P, 4 * P], F32, name="obj_bank", tag="by_sender")
@@ -337,6 +357,7 @@ def tile_compositionalkoopmanoperators_pa_t_kernel(
         particles = mx_tiles(keep, "particles", GRAPHS * PARTICLES)
 
         transpose_receiver(0)
+        copy_waiting(2)
         mx_rounds.append([quantise_unit(grouped_units[0, 0])])
         quantise(columns(particles, 0, GRAPHS * PARTICLES), particles_grouped[:])
         for c in range(F_CHUNKS):
@@ -420,6 +441,7 @@ def tile_compositionalkoopmanoperators_pa_t_kernel(
                 if c == 1:
                     transpose_sender(1)
                     transpose_receiver(1)
+                    copy_waiting(4)
                 if c == 2:
                     quantise_round(1)
 

@@ -27,7 +27,7 @@ WORDS = NF // 2
 RUNNING = 2
 X_BUFS = 7
 SQUARE = 32
-QPOS = ((2, 0), (1, 0))
+QPOS = ((1, 0), (3, 0))
 AHEAD = 2
 
 FLOPS = 2 * NF * NF * (GRAPHS * PARTICLES * PARTICLES + 4 * GRAPHS * PARTICLES)
@@ -44,8 +44,8 @@ def tile_compositionalkoopmanoperators_pa_t_kernel(
         grouped_pool = stack.enter_context(tc.tile_pool(name="grouped_pool", bufs=7))
         q_pool = stack.enter_context(tc.tile_pool(name="q_pool", bufs=4))
         end_pool = stack.enter_context(tc.tile_pool(name="end_pool", bufs=2))
-        flip_psum = stack.enter_context(tc.psum_pool(name="flip_psum", bufs=4))
-        mx_psum = stack.enter_context(tc.psum_pool(name="mx_psum", bufs=2))
+        flip_psum = stack.enter_context(tc.psum_pool(name="flip_psum", bufs=2))
+        mx_psum = stack.enter_context(tc.psum_pool(name="mx_psum", bufs=3))
 
         def mx_tiles(pool, name, cols):
             codes = pool.tile(
@@ -196,9 +196,9 @@ def tile_compositionalkoopmanoperators_pa_t_kernel(
             if r >= ROUNDS:
                 return
             transpose_sender(r)
-            transpose_receiver(r)
-            if not on_vector(r):
-                copy_waiting(4)
+            if on_vector(r):
+                transpose_receiver(r)
+            copy_waiting(2)
 
         mx_rounds = []
 
@@ -263,13 +263,15 @@ def tile_compositionalkoopmanoperators_pa_t_kernel(
             for c in range(F_CHUNKS):
                 sender_bank = sender_products(r, c)
                 receiver_bank = receiver_products(r, c)
-                copy_waiting((2, 1, 1, 0)[c])
+                copy_waiting(2)
                 if r + 1 < ROUNDS:
                     quantise_at(r + 1, c, 0)
                 add_by_sender(r, c, sender_bank)
                 if r + 1 < ROUNDS:
                     quantise_at(r + 1, c, 1)
                 add_by_receiver(r, c, receiver_bank)
+                if c == 1 and 1 < r + 1 < ROUNDS and not on_vector(r + 1):
+                    transpose_receiver(r + 1)
 
         out_rows = out.rearrange("b i n -> (b i) n")
 

@@ -26,6 +26,7 @@ F_CHUNKS = NF // P
 WORDS = NF // 2
 RUNNING = 2
 X_BUFS = 7
+ON_VECTOR_FROM = 4
 SQUARE = 32
 QPOS = ((1, 0), (3, 0))
 AHEAD = 2
@@ -109,7 +110,7 @@ def tile_compositionalkoopmanoperators_pa_t_kernel(
         x_rounds = []
 
         def on_vector(r):
-            return r % 2 == 1
+            return r >= ON_VECTOR_FROM
 
 
         def x_tile():

from contextlib import ExitStack

import concourse.mybir as mybir
from concourse.masks import make_identity

F32 = mybir.dt.float32
BF16 = mybir.dt.bfloat16
I32 = mybir.dt.int32
U32 = mybir.dt.uint32
U8 = mybir.dt.uint8
FP8X4 = mybir.dt.float8_e4m3fn_x4
ALU = mybir.AluOpType
ACT = mybir.ActivationFunctionType

P = 128
PACK = 4
NF = P * PACK
GRAPHS = 4
PARTICLES = 64
HALF_GRAPHS = 2
UNIT_COLS = 512
UNIT_BLOCKS = UNIT_COLS // P
UNIT_SLICES = UNIT_COLS // PARTICLES
ROUNDS = HALF_GRAPHS * PARTICLES * PARTICLES // UNIT_COLS
F_CHUNKS = NF // P
WORDS = NF // 2
RUNNING = 2
X_BUFS = 7
ON_VECTOR_FROM = 4
SQUARE = 32
QPOS = ((1, 0), (3, 0))
AHEAD = 2

FLOPS = 2 * NF * NF * (GRAPHS * PARTICLES * PARTICLES + 4 * GRAPHS * PARTICLES)


def tile_compositionalkoopmanoperators_pa_t_kernel(
    tc, rel_enc, obj, rp_w, rp_b, pp_w, pp_b, out
):
    nc = tc.nc
    with ExitStack() as stack:
        stack.enter_context(tc.manual_schedule())
        keep = stack.enter_context(tc.tile_pool(name="keep", bufs=1))
        x_pool = stack.enter_context(tc.tile_pool(name="x_pool", bufs=2 * X_BUFS))
        grouped_pool = stack.enter_context(tc.tile_pool(name="grouped_pool", bufs=7))
        q_pool = stack.enter_context(tc.tile_pool(name="q_pool", bufs=4))
        end_pool = stack.enter_context(tc.tile_pool(name="end_pool", bufs=2))
        flip_psum = stack.enter_context(tc.psum_pool(name="flip_psum", bufs=2))
        mx_psum = stack.enter_context(tc.psum_pool(name="mx_psum", bufs=3))

        def mx_tiles(pool, name, cols):
            codes = pool.tile(
                [P, cols], U32, name=name + "_codes", tag=name + "_codes", align_bytes=256
            )
            scales = pool.tile(
                [P, cols], U8, name=name + "_scales", tag=name + "_scales", align_bytes=256
            )
            return codes, scales

        def columns(mx, first, count):
            return mx[0][:, first : first + count], mx[1][:, first : first + count]

        def quantise(mx, grouped):
            nc.vector.quantize_mx(out=mx[0].bitcast(FP8X4), scales=mx[1], in_=grouped)

        def mx_pass(bank, stationary, moving, start, stop):
            nc.tensor.matmul_mx(
                out=bank,
                lhsT=stationary[0].bitcast(FP8X4),
                lhsT_scale=stationary[1],
                rhs=moving[0].bitcast(FP8X4),
                rhs_scale=moving[1],
                start=start,
                stop=stop,
            )

        def load_weight(name, rows_by_partition):
            raw = keep.tile([P, PACK * NF], BF16, name=name + "_raw")
            a = rows_by_partition.shape[1]
            nc.sync.dma_start(
                out=raw[:].rearrange("p (a b) -> p a b", a=a), in_=rows_by_partition
            )
            return raw

        def grouped_tile(name):
            return keep.tile([P, NF * PACK], BF16, name=name + "_grouped", align_bytes=64)

        def regroup_weight(grouped, raw, first, count, copy):
            copy(
                out=grouped[:, first * PACK : (first + count) * PACK].rearrange(
                    "p (c i t) -> p c t i", i=4, t=PACK
                ),
                in_=raw[:]
                .rearrange("p (t n) -> p t n", t=PACK)[:, :, first : first + count]
                .rearrange("p t (c i) -> p c t i", i=4),
            )

        def word_order(w):
            return w.rearrange("(u q e) n -> q u (e n)", u=2, e=2)

        def chunk_order(w):
            return w.rearrange("(t p) n -> p t n", p=P)

        def transpose_words(bank, slot, words):
            nc.tensor.transpose(bank[:, slot * P : (slot + 1) * P], words, ident[:])

        by_pair = rel_enc.rearrange("b i j k -> (b i) (j k)")
        by_relation = rel_enc.rearrange("b i j k -> (b i j) k")
        by_half_relation = rel_enc.rearrange("b i j (u k) -> (b i j u) k", u=2)
        x_rounds = []

        def on_vector(r):
            return r >= ON_VECTOR_FROM


        def x_tile():
            return x_pool.tile([P, UNIT_BLOCKS * NF], BF16, name="x_sb", tag="x_sb", align_bytes=64)

        def load_sender_unit(r):
            x_sb = x_tile()
            first = r * UNIT_BLOCKS * NF
            nc.sync.dma_start(out=x_sb[:], in_=by_pair[0:P, first : first + UNIT_BLOCKS * NF])
            return x_sb

        def load_receiver_unit(r):
            x_sb = x_tile()
            first = (ROUNDS + r) * UNIT_COLS
            if on_vector(r):
                for a in range(P // SQUARE):
                    nc.sync.dma_start(
                        out=x_sb[a * SQUARE : (a + 1) * SQUARE, :].rearrange(
                            "p (s k) -> p s k", k=2 * SQUARE
                        ),
                        in_=by_half_relation[
                            2 * first : 2 * (first + UNIT_COLS), 2 * a * SQUARE : 2 * (a + 1) * SQUARE
                        ].rearrange("(s p) k -> p s k", p=SQUARE),
                    )
            else:
                nc.sync.dma_start(
                    out=x_sb[:].rearrange("p (s k) -> p s k", s=UNIT_BLOCKS),
                    in_=by_relation[first : first + UNIT_COLS, :].rearrange("(s p) k -> p s k", p=P),
                )
            return x_sb

        def load_round(r):
            x_rounds.append([load_sender_unit(r), load_receiver_unit(r)])

        def transpose_unit(x_sb, *copies):
            x_words = x_sb[:].bitcast(F32)
            grouped = grouped_pool.tile(
                [P, UNIT_COLS * PACK], BF16, name="grouped", tag="grouped", align_bytes=64
            )
            grouped_words = grouped[:].bitcast(F32)
            for pair in range(UNIT_BLOCKS // 2):
                bank = flip_psum.tile([P, 4 * P], F32, name="flipped", tag="flipped")
                for s in range(2):
                    for u in range(2):
                        first = (2 * pair + s) * WORDS + u * P
                        transpose_words(bank, 2 * s + u, x_words[:, first : first + P])
                waiting_copies.append(
                    lambda copy=copies[pair], pair=pair, bank=bank: copy(
                        out=grouped_words[:, pair * 4 * P : (pair + 1) * 4 * P].rearrange(
                            "q (s c u) -> q s c u", s=2, u=2
                        ),
                        in_=bank[:].rearrange("q (s u c) -> q s c u", s=2, u=2),
                    )
                )
            return grouped

        waiting_copies = []

        def copy_waiting(count):
            for i in range(min(count, len(waiting_copies))):
                waiting_copies.pop(0)()

        def transpose_unit_on_vector(x_sb):
            grouped = grouped_pool.tile(
                [P, UNIT_COLS * PACK], BF16, name="grouped", tag="grouped", align_bytes=64
            )
            nc.vector.transpose(grouped[:].bitcast(F32), x_sb[:].bitcast(F32))
            return grouped

        grouped_units = {}

        def transpose_sender(r):
            first_copy = nc.scalar.copy if on_vector(r) else nc.vector.tensor_copy
            grouped_units[r, 0] = transpose_unit(x_rounds[r][0], first_copy, nc.scalar.copy)

        def transpose_receiver(r):
            if on_vector(r):
                grouped_units[r, 1] = transpose_unit_on_vector(x_rounds[r][1])
            else:
                grouped_units[r, 1] = transpose_unit(x_rounds[r][1], nc.scalar.copy, nc.scalar.copy)

        def transpose_ahead(r):
            r += AHEAD
            if r >= ROUNDS:
                return
            transpose_sender(r)
            if on_vector(r):
                transpose_receiver(r)
            copy_waiting(2)

        mx_rounds = []

        def quantise_unit(grouped):
            mx = mx_tiles(q_pool, "x", UNIT_COLS)
            quantise(columns(mx, 0, UNIT_COLS), grouped[:])
            return mx

        def quantise_at(r, c, pos):
            if c == 0 and pos == 0:
                mx_rounds.append([None, None])
            for kind in (1, 0):
                if QPOS[kind] == (c, pos):
                    mx_rounds[r][kind] = quantise_unit(grouped_units[r, kind])

        def quantise_round(r):
            mx_rounds.append([quantise_unit(grouped_units[r, kind]) for kind in range(2)])

        def sender_products(r, c):
            bank = mx_psum.tile([P, UNIT_COLS], F32, name="by_sender", tag="by_sender")
            moving = columns(mx_rounds[r][0], 0, UNIT_COLS)
            mx_pass(bank[:], columns(wr, c * P, P), moving, True, False)
            mx_pass(bank[:], columns(wi, c * P, P), columns(receivers, 0, UNIT_COLS), False, True)
            return bank

        def receiver_products(r, c):
            bank = mx_psum.tile([P, UNIT_COLS], F32, name="by_receiver", tag="by_receiver")
            graph = r * UNIT_SLICES // PARTICLES
            moving = columns(mx_rounds[r][1], 0, UNIT_COLS)
            mx_pass(bank[:], columns(wr, c * P, P), moving, True, False)
            mx_pass(bank[:], columns(wj, c * P, P), columns(senders[graph], 0, UNIT_COLS), False, True)
            return bank

        def add_by_sender(r, c, bank):
            for s in range(UNIT_BLOCKS):
                for g in range(HALF_GRAPHS):
                    cols = slice(g * PARTICLES, (g + 1) * PARTICLES)
                    sender = g * PARTICLES + r * UNIT_BLOCKS + s
                    nc.vector.scalar_tensor_tensor(
                        out=sums[:, s % RUNNING, c, cols],
                        in0=bank[:, s * P + g * PARTICLES : s * P + (g + 1) * PARTICLES],
                        scalar=neg_send[:, c, sender : sender + 1],
                        in1=sums[:, s % RUNNING, c, cols],
                        op0=ALU.max,
                        op1=ALU.add,
                    )

        def add_by_receiver(r, c, bank):
            effects = end_pool.tile([P, UNIT_COLS], F32, name="effects", tag="effects")
            for i in range(UNIT_SLICES):
                cols = slice(i * PARTICLES, (i + 1) * PARTICLES)
                receiver = r * UNIT_SLICES + i
                nc.scalar.activation(
                    out=effects[:, cols],
                    in_=bank[:, cols],
                    func=ACT.Relu,
                    bias=recv_bias[:, c, receiver : receiver + 1],
                    accum_out=agg_receiver[:, c, receiver : receiver + 1],
                )

        def multiply_round(r):
            for c in range(F_CHUNKS):
                sender_bank = sender_products(r, c)
                receiver_bank = receiver_products(r, c)
                copy_waiting(2)
                if r + 1 < ROUNDS:
                    quantise_at(r + 1, c, 0)
                add_by_sender(r, c, sender_bank)
                if r + 1 < ROUNDS:
                    quantise_at(r + 1, c, 1)
                add_by_receiver(r, c, receiver_bank)
                if c == 1 and 1 < r + 1 < ROUNDS and not on_vector(r + 1):
                    transpose_receiver(r + 1)

        out_rows = out.rearrange("b i n -> (b i) n")

        bias_rows = keep.tile([P, P], BF16, name="bias_rows")
        nc.vector.memset(bias_rows[:], 0.0)
        ident = keep.tile([P, P], F32, name="ident")
        make_identity(nc, ident[:])
        sums = keep.tile([P, RUNNING, F_CHUNKS, P], F32, name="sums")
        nc.gpsimd.memset(sums[:, 0], 0.0)

        obj_sb = keep.tile([P, 2 * NF], BF16, name="obj_sb")
        nc.scalar.dma_start(out=bias_rows[0:F_CHUNKS, :], in_=rp_b.rearrange("(c p) -> c p", p=P))
        x_rounds.append([load_sender_unit(0)])
        nc.sync.dma_start(
            out=obj_sb[:].rearrange("p (h k) -> p h k", h=2),
            in_=obj.rearrange("b i k -> (b i) k").rearrange("(h p) k -> p h k", p=P),
        )
        wr_raw = load_weight("wr", word_order(rp_w[0:NF, :]))
        x_rounds[0].append(load_receiver_unit(0))
        wj_raw = load_weight("wj", word_order(rp_w[2 * NF : 3 * NF, :]))
        wi_raw = load_weight("wi", word_order(rp_w[NF : 2 * NF, :]))
        for r in range(1, X_BUFS):
            load_round(r)
        po_raw = load_weight("po", word_order(pp_w[0:NF, :]))
        pa_raw = load_weight("pa", chunk_order(pp_w[NF : 2 * NF, :]))
        pp_bias = keep.tile([P, NF], BF16, name="pp_bias")
        nc.sync.dma_start(out=pp_bias[:], in_=pp_b.partition_broadcast(P))

        transpose_sender(0)

        copy_waiting(2)

        obj_words = obj_sb[:].bitcast(F32)
        obj_bank = mx_psum.tile([P, 4 * P], F32, name="obj_bank", tag="by_sender")
        for half in range(2):
            for u in range(2):
                first = half * WORDS + u * P
                transpose_words(obj_bank, 2 * half + u, obj_words[:, first : first + P])
        particles_grouped = keep.tile(
            [P, GRAPHS * PARTICLES * PACK], BF16, name="particles_grouped", align_bytes=64
        )
        particle_words = particles_grouped[:].bitcast(F32)
        nc.scalar.copy(
            out=particle_words.rearrange("q (h c u) -> q h c u", h=2, u=2),
            in_=obj_bank[:].rearrange("q (h u c) -> q h c u", h=2, u=2),
        )

        bias_f32 = keep.tile([P, P], F32, name="bias_f32")
        nc.vector.tensor_copy(out=bias_f32[:], in_=bias_rows[:])
        bias_bank = mx_psum.tile([P, 4 * P], F32, name="bias_bank", tag="by_receiver")
        transpose_words(bias_bank, 0, bias_f32[:])
        rp_bias = keep.tile([P, F_CHUNKS], F32, name="rp_bias")
        neg_rp_bias = keep.tile([P, F_CHUNKS], F32, name="neg_rp_bias")
        nc.scalar.copy(out=rp_bias[:], in_=bias_bank[:, 0:F_CHUNKS])
        nc.scalar.mul(neg_rp_bias[:], rp_bias[:], -1.0)

        def repeated(name, first, count):
            times = UNIT_COLS // count
            mx = mx_tiles(keep, name, UNIT_COLS)
            for to, source in zip(mx, columns(particles, first, count)):
                words = source.bitcast(I32)
                nc.vector.tensor_copy(
                    out=to[:].bitcast(I32).rearrange("q (r w) -> q r w", r=times),
                    in_=words.unsqueeze(1).to_broadcast([P, times, words.shape[1]]),
                )
            return mx

        weights = {}

        def weight_tiles(name, raw):
            weights[name] = (raw, grouped_tile(name), mx_tiles(keep, name, NF))
            return weights[name][2]

        def regroup_chunk(name, c, copy):
            raw, grouped, mx = weights[name]
            regroup_weight(grouped, raw, c * P, P, copy)

        def quantise_chunk(name, c):
            raw, grouped, mx = weights[name]
            quantise(columns(mx, c * P, P), grouped[:, c * P * PACK : (c + 1) * P * PACK])

        wr = weight_tiles("wr", wr_raw)
        wj = weight_tiles("wj", wj_raw)
        wi = weight_tiles("wi", wi_raw)
        particles = mx_tiles(keep, "particles", GRAPHS * PARTICLES)

        transpose_receiver(0)
        copy_waiting(2)
        mx_rounds.append([quantise_unit(grouped_units[0, 0])])
        quantise(columns(particles, 0, GRAPHS * PARTICLES), particles_grouped[:])
        for c in range(F_CHUNKS):
            regroup_chunk("wr", c, nc.vector.tensor_copy)
        for c in range(F_CHUNKS):
            regroup_chunk("wj", c, nc.scalar.copy)
        receivers = repeated("receivers", 0, P)
        senders = [
            repeated("senders%d" % g, P + g * PARTICLES, PARTICLES) for g in range(HALF_GRAPHS)
        ]
        mx_rounds[0].append(quantise_unit(grouped_units[0, 1]))
        quantise_chunk("wr", 0)
        regroup_chunk("wi", 0, nc.vector.tensor_copy)
        for name in ("wj", "wi"):
            quantise_chunk(name, 0)

        neg_send = keep.tile([P, F_CHUNKS, P], F32, name="neg_send")
        recv_bias = keep.tile([P, F_CHUNKS, P], F32, name="recv_bias")
        neg_send_sum = keep.tile([P, F_CHUNKS, HALF_GRAPHS], F32, name="neg_send_sum")
        agg_receiver = keep.tile([P, F_CHUNKS, P], F32, name="agg_receiver")

        def particle_products(c):
            send_bank = flip_psum.tile([P, 4 * P], F32, name="send_bank", tag="flipped")
            mx_pass(send_bank[:, 0:P], columns(wj, c * P, P), columns(particles, 0, P), True, True)
            recv_bank = flip_psum.tile([P, 4 * P], F32, name="recv_bank", tag="flipped")
            mx_pass(recv_bank[:, 0:P], columns(wi, c * P, P), columns(particles, P, P), True, True)
            for g in range(HALF_GRAPHS):
                cols = slice(g * PARTICLES, (g + 1) * PARTICLES)
                nc.scalar.activation(
                    out=neg_send[:, c, cols],
                    in_=send_bank[:, cols],
                    func=ACT.Identity,
                    scale=-1.0,
                    bias=neg_rp_bias[:, c : c + 1],
                    accum_out=neg_send_sum[:, c, g : g + 1],
                )
            nc.scalar.activation(
                out=sums[:, 1, c, :].rearrange("p (b n) -> p b n", b=HALF_GRAPHS),
                in_=neg_send_sum[:, c, :].unsqueeze(2).to_broadcast([P, HALF_GRAPHS, PARTICLES]),
                func=ACT.Copy,
                scale=-1.0,
            )
            nc.scalar.activation(
                out=recv_bias[:, c, :],
                in_=recv_bank[:, 0:P],
                func=ACT.Identity,
                bias=rp_bias[:, c : c + 1],
            )

        def prepare_chunk(c):
            regroup_chunk("wi", c, nc.vector.tensor_copy)
            for name in ("wr", "wj", "wi"):
                quantise_chunk(name, c)

        particle_products(0)
        prepare_chunk(1)

        po = weight_tiles("po", po_raw)
        pa = weight_tiles("pa", pa_raw)
        chores = []
        for name in ("po", "pa"):
            for c in range(F_CHUNKS):
                chores.append(lambda name=name, c=c: regroup_chunk(name, c, nc.scalar.copy))
        for name in ("po", "pa"):
            chores.append(lambda name=name: quantise_whole(name))

        def quantise_whole(name):
            raw, grouped, mx = weights[name]
            quantise(columns(mx, 0, NF), grouped[:])

        def first_round():
            for c in range(F_CHUNKS):
                sender_bank = sender_products(0, c)
                receiver_bank = receiver_products(0, c)
                if c + 1 < F_CHUNKS:
                    particle_products(c + 1)
                add_by_sender(0, c, sender_bank)
                if c + 2 < F_CHUNKS:
                    prepare_chunk(c + 2)
                add_by_receiver(0, c, receiver_bank)
                if c == 1:
                    transpose_sender(1)
                    transpose_receiver(1)
                    copy_waiting(4)
                if c == 2:
                    quantise_round(1)

        for r in range(ROUNDS):
            if r == 0:
                first_round()
            else:
                multiply_round(r)
            transpose_ahead(r)
            if r + X_BUFS < ROUNDS:
                load_round(r + X_BUFS)
            if r >= ROUNDS - len(chores) - 1 and chores:
                chores.pop(0)()

        banks = []
        for half in range(2):
            bank = flip_psum.tile([P, NF], F32, name="particle", tag="flipped")
            mx_pass(bank[:], columns(particles, half * P, P), columns(po, 0, NF), True, False)
            banks.append(bank)
        agg = [
            end_pool.tile([P, P, PACK], BF16, name="agg%d" % half, tag="agg%d" % half, align_bytes=64)
            for half in range(2)
        ]
        nc.scalar.copy(out=agg[1][:], in_=agg_receiver[:].rearrange("p c n -> p n c"))
        nc.vector.tensor_tensor(
            out=agg[0][:],
            in0=sums[:, 0].rearrange("p c n -> p n c"),
            in1=sums[:, 1].rearrange("p c n -> p n c"),
            op=ALU.add,
        )
        agg_mx = [mx_tiles(keep, "agg%d" % half, P) for half in range(2)]
        for half in (1, 0):
            quantise(columns(agg_mx[half], 0, P), agg[half][:].rearrange("p c t -> p (c t)"))
        half_cols = NF // 2
        for half in (1, 0):
            mx_pass(banks[half][:], columns(agg_mx[half], 0, P), columns(pa, 0, NF), False, True)
            for part in range(2):
                cols = slice(part * half_cols, (part + 1) * half_cols)
                result = keep.tile([P, half_cols], F32, name="result%d%d" % (half, part))
                nc.vector.tensor_tensor(
                    out=result[:], in0=banks[half][:, cols], in1=pp_bias[:, cols], op=ALU.add
                )
                nc.scalar.activation(out=result[:], in_=result[:], func=ACT.Relu)
                nc.sync.dma_start(out=out_rows[half * P : (half + 1) * P, cols], in_=result[:])
